import numpy as np
import ml_dtypes

BF16 = ml_dtypes.bfloat16


def bf(x):
    return np.asarray(x, np.float32).astype(BF16)


def f32(x):
    return np.asarray(x, np.float32)


def f64(x):
    return np.asarray(x).astype(np.float64)


def striped(idx):
    return np.tile(idx.reshape(-1, 16).T, (8, 1))


C, F, S, N = 256, 128, 4096, 2048
EPS = 1e-5
ERF_TERMS, ERF_LIM = 150, 6.0


def erf(a):
    ac = np.clip(a, -ERF_LIM, ERF_LIM)
    term = ac.copy()
    tot = ac.copy()
    for t in range(1, ERF_TERMS):
        term = term * (2.0 * ac * ac) / (2.0 * t + 1.0)
        tot = tot + term
    val = 2.0 / np.sqrt(np.pi) * np.exp(-ac * ac) * tot
    return np.where(np.abs(a) > ERF_LIM, np.sign(a), val)


def setup_inputs():
    return {
        "base": f32(np.random.standard_normal((C, S))),
        "x": f32(np.random.standard_normal((C, N))),
        "ln_w": f32(1.0 + 0.1 * np.random.standard_normal((C, 1))),
        "ln_b": f32(0.1 * np.random.standard_normal((C, 1))),
        "w1": bf(np.random.standard_normal((C, F)) / np.sqrt(C)),
        "b1": f32(0.1 * np.random.standard_normal((F, 1))),
        "w2": bf(np.random.standard_normal((F, C)) / np.sqrt(F)),
        "b2": f32(0.1 * np.random.standard_normal((C, 1))),
        "offs": striped(np.random.permutation(S)[:N]),
    }


def reference(base, x, ln_w, ln_b, w1, b1, w2, b2, offs):
    idx = offs[:16].T.reshape(-1)
    xr = np.maximum(f64(x), 0.0)
    mu = xr.mean(axis=0, keepdims=True)
    var = ((xr - mu) ** 2).mean(axis=0, keepdims=True)
    z = (xr - mu) / np.sqrt(var + EPS) * f64(ln_w) + f64(ln_b)
    a = f64(w1).T @ z + f64(b1)
    h = 0.5 * a * (1.0 + erf(a / np.sqrt(2.0)))
    f = f64(w2).T @ h
    r = xr + f64(b2)
    out = f64(base).copy()
    out[:, idx] = f + r
    return out

@@ -1,0 +1,115 @@
+import concourse.mybir as mybir
+
+F32 = mybir.dt.float32
+BF16 = mybir.dt.bfloat16
+U16 = mybir.dt.uint16
+ACT = mybir.ActivationFunctionType
+ALU = mybir.AluOpType
+
+P = 128
+C, F, S, N = 256, 128, 4096, 2048
+CB = C // P
+CHUNK = 512
+NCHUNK = N // CHUNK
+EPS = 1e-5
+
+FLOPS = 2 * N * C * F * 2
+
+
+def tile_molecularretnet_kernel(tc, base, x, ln_w, ln_b, w1, b1, w2, b2, offs, out):
+    nc = tc.nc
+    with (
+        tc.tile_pool(name="held", bufs=1) as held,
+        tc.tile_pool(name="work", bufs=2) as work,
+        tc.psum_pool(name="stat", bufs=2) as stat,
+        tc.psum_pool(name="bank", bufs=4) as bank,
+    ):
+        X = [held.tile([P, N], F32, name=f"X{cb}") for cb in range(CB)]
+        for t in range(NCHUNK):
+            for cb in range(CB):
+                nc.sync.dma_start(
+                    X[cb][:, t * CHUNK : (t + 1) * CHUNK],
+                    x[cb * P : (cb + 1) * P, t * CHUNK : (t + 1) * CHUNK],
+                )
+        offsets = held.tile([P, N // 16], U16, name="offsets")
+        nc.sync.dma_start(offsets[:], offs)
+        window = [held.tile([P, S], F32, name=f"window{cb}") for cb in range(CB)]
+        for cb in range(CB):
+            nc.sync.dma_start(window[cb][:], base[cb * P : (cb + 1) * P, :])
+
+        w1_sb = held.tile([P, CB, F], BF16, name="w1_sb")
+        nc.scalar.dma_start(w1_sb[:], w1.rearrange("(b p) k -> p b k", p=P))
+        w2_sb = held.tile([P, C], BF16, name="w2_sb")
+        nc.scalar.dma_start(w2_sb[:], w2)
+        rows = held.tile([1, 7 * P], F32, name="rows")
+        nc.scalar.dma_start(rows[0:1, 0 : 2 * P], ln_w.rearrange("c o -> o c"))
+        nc.scalar.dma_start(rows[0:1, 2 * P : 4 * P], ln_b.rearrange("c o -> o c"))
+        nc.scalar.dma_start(rows[0:1, 4 * P : 6 * P], b2.rearrange("c o -> o c"))
+        nc.scalar.dma_start(rows[0:1, 6 * P : 7 * P], b1.rearrange("c o -> o c"))
+
+        avg_f32 = held.tile([P, P], F32, name="avg_f32")
+        nc.gpsimd.memset(avg_f32[:], 1.0 / C)
+        avg_bf16 = held.tile([P, P], BF16, name="avg_bf16")
+        nc.gpsimd.memset(avg_bf16[:], 1.0 / C)
+        eps_col = held.tile([P, 1], F32, name="eps_col")
+        nc.gpsimd.memset(eps_col[:], EPS)
+        one = held.tile([1, 1], F32, name="one")
+        nc.gpsimd.memset(one[:], 1.0)
+
+        cols_ps = bank.tile([P, 7], F32, name="cols_ps", tag="bank")
+        for k in range(7):
+            nc.tensor.matmul(
+                cols_ps[:, k : k + 1], rows[0:1, k * P : (k + 1) * P], one[:], start=True, stop=True
+            )
+        cols = held.tile([P, 7], F32, name="cols")
+        nc.vector.tensor_copy(cols[:], cols_ps[:])
+        ln_w_col = [cols[:, cb : cb + 1] for cb in range(CB)]
+        ln_b_col = [cols[:, 2 + cb : 3 + cb] for cb in range(CB)]
+        b2_col = [cols[:, 4 + cb : 5 + cb] for cb in range(CB)]
+        b1_col = cols[:, 6:7]
+
+        a_ps = []
+        for t in range(NCHUNK):
+            tok = slice(t * CHUNK, (t + 1) * CHUNK)
+            for cb in range(CB):
+                nc.scalar.activation(X[cb][:, tok], X[cb][:, tok], ACT.Relu)
+            both = work.tile([P, CHUNK], F32, name="both")
+            nc.gpsimd.tensor_tensor(both[:], X[0][:, tok], X[1][:, tok], ALU.add)
+            mu_ps = stat.tile([P, CHUNK], F32, name="mu_ps")
+            nc.tensor.matmul(mu_ps[:], avg_f32[:], both[:], start=True, stop=True)
+            centred = [work.tile([P, CHUNK], F32, name=f"centred{cb}") for cb in range(CB)]
+            squared = [work.tile([P, CHUNK], BF16, name=f"squared{cb}") for cb in range(CB)]
+            var_ps = stat.tile([P, CHUNK], F32, name="var_ps")
+            for cb in range(CB):
+                nc.vector.tensor_tensor(centred[cb][:], X[cb][:, tok], mu_ps[:], ALU.subtract)
+                nc.scalar.activation(squared[cb][:], centred[cb][:], ACT.Square)
+                nc.tensor.matmul(
+                    var_ps[:], avg_bf16[:], squared[cb][:], start=(cb == 0), stop=(cb == CB - 1)
+                )
+            rstd = work.tile([P, CHUNK], F32, name="rstd")
+            nc.scalar.activation(rstd[:], var_ps[:], ACT.Abs_reciprocal_sqrt, bias=eps_col[:])
+            a_ps.append(bank.tile([P, CHUNK], F32, name=f"a_ps{t}", tag="bank"))
+            for cb in range(CB):
+                normed = work.tile([P, CHUNK], F32, name=f"normed{cb}")
+                nc.vector.tensor_tensor(normed[:], centred[cb][:], rstd[:], ALU.mult)
+                z = work.tile([P, CHUNK], BF16, name=f"z{cb}")
+                nc.gpsimd.tensor_scalar(z[:], normed[:], ln_w_col[cb], ln_b_col[cb], ALU.mult, ALU.add)
+                nc.tensor.matmul(a_ps[t][:], w1_sb[:, cb, :], z[:], start=(cb == 0), stop=(cb == CB - 1))
+
+        h = held.tile([P, N], BF16, name="h")
+        f_b2 = [held.tile([P, N], F32, name=f"f_b2_{cb}") for cb in range(CB)]
+        for t in range(NCHUNK):
+            tok = slice(t * CHUNK, (t + 1) * CHUNK)
+            nc.scalar.activation(h[:, tok], a_ps[t][:], ACT.Gelu, bias=b1_col)
+            f_ps = bank.tile([P, CHUNK], F32, name="f_ps0", tag="bank")
+            nc.tensor.matmul(f_ps[:], w2_sb[:, 0:P], h[:, tok], start=True, stop=True)
+            nc.vector.tensor_scalar(f_b2[0][:, tok], f_ps[:], b2_col[0], None, ALU.add)
+        for t in range(NCHUNK):
+            tok = slice(t * CHUNK, (t + 1) * CHUNK)
+            f_ps = bank.tile([P, CHUNK], F32, name="f_ps1", tag="bank")
+            nc.tensor.matmul(f_ps[:], w2_sb[:, P : 2 * P], h[:, tok], start=True, stop=True)
+            nc.scalar.activation(f_b2[1][:, tok], f_ps[:], ACT.Identity, bias=b2_col[1])
+
+        for cb in range(CB):
+            nc.vector.tensor_tensor(window[cb][:].indirect(offsets[:]), f_b2[cb][:], X[cb][:], ALU.add)
+            nc.sync.dma_start(out[cb * P : (cb + 1) * P, :], window[cb][:])

@@ -1,4 +1,5 @@
 import concourse.mybir as mybir
+from concourse.masks import make_identity
 
 F32 = mybir.dt.float32
 BF16 = mybir.dt.bfloat16
@@ -12,40 +13,39 @@ CB = C // P
 CHUNK = 512
 NCHUNK = N // CHUNK
 EPS = 1e-5
+NROWS = 7
 
 FLOPS = 2 * N * C * F * 2
 
 
 def tile_molecularretnet_kernel(tc, base, x, ln_w, ln_b, w1, b1, w2, b2, offs, out):
     nc = tc.nc
+    chunks = [slice(t * CHUNK, (t + 1) * CHUNK) for t in range(NCHUNK)]
+    blocks = [slice(cb * P, (cb + 1) * P) for cb in range(CB)]
     with (
         tc.tile_pool(name="held", bufs=1) as held,
-        tc.tile_pool(name="work", bufs=2) as work,
-        tc.psum_pool(name="stat", bufs=2) as stat,
-        tc.psum_pool(name="bank", bufs=4) as bank,
+        tc.psum_pool(name="psum", bufs=4) as psum,
     ):
-        X = [held.tile([P, N], F32, name=f"X{cb}") for cb in range(CB)]
-        for t in range(NCHUNK):
+        w1_sb = held.tile([P, CB, F], BF16, name="w1_sb")
+        nc.sync.dma_start(w1_sb[:], w1.rearrange("(b p) k -> p b k", p=P))
+        w2_sb = held.tile([P, C], BF16, name="w2_sb")
+        nc.sync.dma_start(w2_sb[:], w2)
+        rows = held.tile([NROWS, P], F32, name="rows")
+        nc.sync.dma_start(rows[0:2, :], ln_w.rearrange("(r p) o -> r (p o)", p=P))
+        nc.sync.dma_start(rows[2:4, :], ln_b.rearrange("(r p) o -> r (p o)", p=P))
+        nc.sync.dma_start(rows[4:6, :], b2.rearrange("(r p) o -> r (p o)", p=P))
+        nc.sync.dma_start(rows[6:7, :], b1.rearrange("(r p) o -> r (p o)", p=P))
+
+        x_sb = [held.tile([P, N], F32, name=f"x_sb{cb}") for cb in range(CB)]
+        x_queue = [nc.sync, nc.scalar]
+        for tok in chunks:
             for cb in range(CB):
-                nc.sync.dma_start(
-                    X[cb][:, t * CHUNK : (t + 1) * CHUNK],
-                    x[cb * P : (cb + 1) * P, t * CHUNK : (t + 1) * CHUNK],
-                )
+                x_queue[cb].dma_start(x_sb[cb][:, tok], x[blocks[cb], tok])
         offsets = held.tile([P, N // 16], U16, name="offsets")
         nc.sync.dma_start(offsets[:], offs)
         window = [held.tile([P, S], F32, name=f"window{cb}") for cb in range(CB)]
         for cb in range(CB):
-            nc.sync.dma_start(window[cb][:], base[cb * P : (cb + 1) * P, :])
-
-        w1_sb = held.tile([P, CB, F], BF16, name="w1_sb")
-        nc.scalar.dma_start(w1_sb[:], w1.rearrange("(b p) k -> p b k", p=P))
-        w2_sb = held.tile([P, C], BF16, name="w2_sb")
-        nc.scalar.dma_start(w2_sb[:], w2)
-        rows = held.tile([1, 7 * P], F32, name="rows")
-        nc.scalar.dma_start(rows[0:1, 0 : 2 * P], ln_w.rearrange("c o -> o c"))
-        nc.scalar.dma_start(rows[0:1, 2 * P : 4 * P], ln_b.rearrange("c o -> o c"))
-        nc.scalar.dma_start(rows[0:1, 4 * P : 6 * P], b2.rearrange("c o -> o c"))
-        nc.scalar.dma_start(rows[0:1, 6 * P : 7 * P], b1.rearrange("c o -> o c"))
+            nc.sync.dma_start(window[cb][:], base[blocks[cb], :])
 
         avg_f32 = held.tile([P, P], F32, name="avg_f32")
         nc.gpsimd.memset(avg_f32[:], 1.0 / C)
@@ -53,63 +53,79 @@ def tile_molecularretnet_kernel(tc, base, x, ln_w, ln_b, w1, b1, w2, b2, offs, o
         nc.gpsimd.memset(avg_bf16[:], 1.0 / C)
         eps_col = held.tile([P, 1], F32, name="eps_col")
         nc.gpsimd.memset(eps_col[:], EPS)
-        one = held.tile([1, 1], F32, name="one")
-        nc.gpsimd.memset(one[:], 1.0)
+        identity = held.tile([NROWS, NROWS], F32, name="identity")
+        make_identity(nc, identity[:])
+        warm = held.tile([P, 1], F32, name="warm")
+        nc.scalar.activation(warm[:], eps_col[:], ACT.Abs_reciprocal_sqrt)
 
-        cols_ps = bank.tile([P, 7], F32, name="cols_ps", tag="bank")
-        for k in range(7):
-            nc.tensor.matmul(
-                cols_ps[:, k : k + 1], rows[0:1, k * P : (k + 1) * P], one[:], start=True, stop=True
+
+        X = [held.tile([P, N], F32, name=f"X{cb}") for cb in range(CB)]
+        both = held.tile([P, N], F32, name="both")
+        mu_ps = [psum.tile([P, CHUNK], F32, name=f"mu_ps{t}", tag="mu_a") for t in range(NCHUNK)]
+        for t, tok in enumerate(chunks):
+            nc.vector.tensor_scalar_max(X[0][:, tok], x_sb[0][:, tok], 0.0)
+            nc.scalar.activation(X[1][:, tok], x_sb[1][:, tok], ACT.Relu)
+            nc.vector.scalar_tensor_tensor(
+                both[:, tok], x_sb[1][:, tok], 0.0, X[0][:, tok], ALU.max, ALU.add
             )
-        cols = held.tile([P, 7], F32, name="cols")
-        nc.vector.tensor_copy(cols[:], cols_ps[:])
+            nc.tensor.matmul(mu_ps[t][:], avg_f32[:], both[:, tok], start=True, stop=True)
+
+        cols_ps = psum.tile([P, NROWS], F32, name="cols_ps", tag="var_f")
+        nc.tensor.matmul(cols_ps[:], rows[:], identity[:], start=True, stop=True)
+        cols = held.tile([P, NROWS], F32, name="cols")
+        nc.scalar.copy(cols[:], cols_ps[:])
         ln_w_col = [cols[:, cb : cb + 1] for cb in range(CB)]
         ln_b_col = [cols[:, 2 + cb : 3 + cb] for cb in range(CB)]
         b2_col = [cols[:, 4 + cb : 5 + cb] for cb in range(CB)]
         b1_col = cols[:, 6:7]
 
-        a_ps = []
-        for t in range(NCHUNK):
-            tok = slice(t * CHUNK, (t + 1) * CHUNK)
-            for cb in range(CB):
-                nc.scalar.activation(X[cb][:, tok], X[cb][:, tok], ACT.Relu)
-            both = work.tile([P, CHUNK], F32, name="both")
-            nc.gpsimd.tensor_tensor(both[:], X[0][:, tok], X[1][:, tok], ALU.add)
-            mu_ps = stat.tile([P, CHUNK], F32, name="mu_ps")
-            nc.tensor.matmul(mu_ps[:], avg_f32[:], both[:], start=True, stop=True)
-            centred = [work.tile([P, CHUNK], F32, name=f"centred{cb}") for cb in range(CB)]
-            squared = [work.tile([P, CHUNK], BF16, name=f"squared{cb}") for cb in range(CB)]
-            var_ps = stat.tile([P, CHUNK], F32, name="var_ps")
-            for cb in range(CB):
-                nc.vector.tensor_tensor(centred[cb][:], X[cb][:, tok], mu_ps[:], ALU.subtract)
-                nc.scalar.activation(squared[cb][:], centred[cb][:], ACT.Square)
-                nc.tensor.matmul(
-                    var_ps[:], avg_bf16[:], squared[cb][:], start=(cb == 0), stop=(cb == CB - 1)
+        centred = [held.tile([P, N], F32, name=f"centred{cb}") for cb in range(CB)]
+        squared = [held.tile([P, N], BF16, name=f"squared{cb}") for cb in range(CB)]
+        var_ps = [psum.tile([P, CHUNK], F32, name=f"var_ps{t}", tag="var_f") for t in range(NCHUNK)]
+        rstd = held.tile([P, N], F32, name="rstd")
+        for t in range(NCHUNK + 1):
+            if t < NCHUNK:
+                tok = chunks[t]
+                for cb in range(CB):
+                    nc.vector.tensor_tensor(centred[cb][:, tok], X[cb][:, tok], mu_ps[t][:], ALU.subtract)
+                nc.gpsimd.tensor_tensor(squared[0][:, tok], centred[0][:, tok], centred[0][:, tok], ALU.mult)
+                nc.scalar.activation(squared[1][:, tok], centred[1][:, tok], ACT.Square)
+                for cb in range(CB):
+                    nc.tensor.matmul(
+                        var_ps[t][:], avg_bf16[:], squared[cb][:, tok], start=(cb == 0), stop=(cb == CB - 1)
+                    )
+            if t > 0:
+                nc.scalar.activation(
+                    rstd[:, chunks[t - 1]], var_ps[t - 1][:], ACT.Abs_reciprocal_sqrt, bias=eps_col[:]
                 )
-            rstd = work.tile([P, CHUNK], F32, name="rstd")
-            nc.scalar.activation(rstd[:], var_ps[:], ACT.Abs_reciprocal_sqrt, bias=eps_col[:])
-            a_ps.append(bank.tile([P, CHUNK], F32, name=f"a_ps{t}", tag="bank"))
+
+        normed = [held.tile([P, N], F32, name=f"normed{cb}") for cb in range(CB)]
+        z = [held.tile([P, N], BF16, name=f"z{cb}") for cb in range(CB)]
+        z_engine = [nc.gpsimd, nc.vector]
+        a_ps = [psum.tile([P, CHUNK], F32, name=f"a_ps{t}", tag="mu_a") for t in range(NCHUNK)]
+        for t, tok in enumerate(chunks):
             for cb in range(CB):
-                normed = work.tile([P, CHUNK], F32, name=f"normed{cb}")
-                nc.vector.tensor_tensor(normed[:], centred[cb][:], rstd[:], ALU.mult)
-                z = work.tile([P, CHUNK], BF16, name=f"z{cb}")
-                nc.gpsimd.tensor_scalar(z[:], normed[:], ln_w_col[cb], ln_b_col[cb], ALU.mult, ALU.add)
-                nc.tensor.matmul(a_ps[t][:], w1_sb[:, cb, :], z[:], start=(cb == 0), stop=(cb == CB - 1))
+                nc.vector.tensor_tensor(normed[cb][:, tok], centred[cb][:, tok], rstd[:, tok], ALU.mult)
+                z_engine[cb].tensor_scalar(
+                    z[cb][:, tok], normed[cb][:, tok], ln_w_col[cb], ln_b_col[cb], ALU.mult, ALU.add
+                )
+            for cb in range(CB):
+                nc.tensor.matmul(
+                    a_ps[t][:], w1_sb[:, cb, :], z[cb][:, tok], start=(cb == 0), stop=(cb == CB - 1)
+                )
 
         h = held.tile([P, N], BF16, name="h")
         f_b2 = [held.tile([P, N], F32, name=f"f_b2_{cb}") for cb in range(CB)]
-        for t in range(NCHUNK):
-            tok = slice(t * CHUNK, (t + 1) * CHUNK)
+        for t, tok in enumerate(chunks):
             nc.scalar.activation(h[:, tok], a_ps[t][:], ACT.Gelu, bias=b1_col)
-            f_ps = bank.tile([P, CHUNK], F32, name="f_ps0", tag="bank")
-            nc.tensor.matmul(f_ps[:], w2_sb[:, 0:P], h[:, tok], start=True, stop=True)
+            f_ps = psum.tile([P, CHUNK], F32, name="f_ps0", tag="var_f")
+            nc.tensor.matmul(f_ps[:], w2_sb[:, blocks[0]], h[:, tok], start=True, stop=True)
             nc.vector.tensor_scalar(f_b2[0][:, tok], f_ps[:], b2_col[0], None, ALU.add)
-        for t in range(NCHUNK):
-            tok = slice(t * CHUNK, (t + 1) * CHUNK)
-            f_ps = bank.tile([P, CHUNK], F32, name="f_ps1", tag="bank")
-            nc.tensor.matmul(f_ps[:], w2_sb[:, P : 2 * P], h[:, tok], start=True, stop=True)
+        for tok in chunks:
+            f_ps = psum.tile([P, CHUNK], F32, name="f_ps1", tag="var_f")
+            nc.tensor.matmul(f_ps[:], w2_sb[:, blocks[1]], h[:, tok], start=True, stop=True)
             nc.scalar.activation(f_b2[1][:, tok], f_ps[:], ACT.Identity, bias=b2_col[1])
 
         for cb in range(CB):
             nc.vector.tensor_tensor(window[cb][:].indirect(offsets[:]), f_b2[cb][:], X[cb][:], ALU.add)
-            nc.sync.dma_start(out[cb * P : (cb + 1) * P, :], window[cb][:])
+            nc.sync.dma_start(out[blocks[cb], :], window[cb][:])

@@ -26,6 +26,11 @@ def tile_molecularretnet_kernel(tc, base, x, ln_w, ln_b, w1, b1, w2, b2, offs, o
         tc.tile_pool(name="held", bufs=1) as held,
         tc.psum_pool(name="psum", bufs=4) as psum,
     ):
+        x_sb = [held.tile([P, N], F32, name=f"x_sb{cb}") for cb in range(CB)]
+        x_queue = [nc.sync, nc.scalar]
+        for tok in chunks:
+            for cb in range(CB):
+                x_queue[cb].dma_start(x_sb[cb][:, tok], x[blocks[cb], tok])
         w1_sb = held.tile([P, CB, F], BF16, name="w1_sb")
         nc.sync.dma_start(w1_sb[:], w1.rearrange("(b p) k -> p b k", p=P))
         w2_sb = held.tile([P, C], BF16, name="w2_sb")
@@ -35,12 +40,6 @@ def tile_molecularretnet_kernel(tc, base, x, ln_w, ln_b, w1, b1, w2, b2, offs, o
         nc.sync.dma_start(rows[2:4, :], ln_b.rearrange("(r p) o -> r (p o)", p=P))
         nc.sync.dma_start(rows[4:6, :], b2.rearrange("(r p) o -> r (p o)", p=P))
         nc.sync.dma_start(rows[6:7, :], b1.rearrange("(r p) o -> r (p o)", p=P))
-
-        x_sb = [held.tile([P, N], F32, name=f"x_sb{cb}") for cb in range(CB)]
-        x_queue = [nc.sync, nc.scalar]
-        for tok in chunks:
-            for cb in range(CB):
-                x_queue[cb].dma_start(x_sb[cb][:, tok], x[blocks[cb], tok])
         offsets = held.tile([P, N // 16], U16, name="offsets")
         nc.sync.dma_start(offsets[:], offs)
         window = [held.tile([P, S], F32, name=f"window{cb}") for cb in range(CB)]
@@ -79,6 +78,16 @@ def tile_molecularretnet_kernel(tc, base, x, ln_w, ln_b, w1, b1, w2, b2, offs, o
         b2_col = [cols[:, 4 + cb : 5 + cb] for cb in range(CB)]
         b1_col = cols[:, 6:7]
 
+        w1_f32 = held.tile([P, CB, F], F32, name="w1_f32")
+        nc.gpsimd.tensor_copy(w1_f32[:], w1_sb[:])
+        shift_ps = psum.tile([P, 1], F32, name="shift_ps", tag="var_f")
+        for cb in range(CB):
+            nc.tensor.matmul(
+                shift_ps[:], w1_f32[:, cb, :], ln_b_col[cb], start=(cb == 0), stop=(cb == CB - 1)
+            )
+        a_bias = held.tile([P, 1], F32, name="a_bias")
+        nc.scalar.activation(a_bias[:], shift_ps[:], ACT.Identity, bias=b1_col)
+
         centred = [held.tile([P, N], F32, name=f"centred{cb}") for cb in range(CB)]
         squared = [held.tile([P, N], BF16, name=f"squared{cb}") for cb in range(CB)]
         var_ps = [psum.tile([P, CHUNK], F32, name=f"var_ps{t}", tag="var_f") for t in range(NCHUNK)]
@@ -86,8 +95,10 @@ def tile_molecularretnet_kernel(tc, base, x, ln_w, ln_b, w1, b1, w2, b2, offs, o
         for t in range(NCHUNK + 1):
             if t < NCHUNK:
                 tok = chunks[t]
-                for cb in range(CB):
-                    nc.vector.tensor_tensor(centred[cb][:, tok], X[cb][:, tok], mu_ps[t][:], ALU.subtract)
+                nc.vector.tensor_tensor(centred[0][:, tok], X[0][:, tok], mu_ps[t][:], ALU.subtract)
+                nc.vector.scalar_tensor_tensor(
+                    centred[1][:, tok], x_sb[1][:, tok], 0.0, mu_ps[t][:], ALU.max, ALU.subtract
+                )
                 nc.gpsimd.tensor_tensor(squared[0][:, tok], centred[0][:, tok], centred[0][:, tok], ALU.mult)
                 nc.scalar.activation(squared[1][:, tok], centred[1][:, tok], ACT.Square)
                 for cb in range(CB):
@@ -99,17 +110,13 @@ def tile_molecularretnet_kernel(tc, base, x, ln_w, ln_b, w1, b1, w2, b2, offs, o
                     rstd[:, chunks[t - 1]], var_ps[t - 1][:], ACT.Abs_reciprocal_sqrt, bias=eps_col[:]
                 )
 
-        normed = [held.tile([P, N], F32, name=f"normed{cb}") for cb in range(CB)]
         z = [held.tile([P, N], BF16, name=f"z{cb}") for cb in range(CB)]
-        z_engine = [nc.gpsimd, nc.vector]
         a_ps = [psum.tile([P, CHUNK], F32, name=f"a_ps{t}", tag="mu_a") for t in range(NCHUNK)]
         for t, tok in enumerate(chunks):
             for cb in range(CB):
-                nc.vector.tensor_tensor(normed[cb][:, tok], centred[cb][:, tok], rstd[:, tok], ALU.mult)
-                z_engine[cb].tensor_scalar(
-                    z[cb][:, tok], normed[cb][:, tok], ln_w_col[cb], ln_b_col[cb], ALU.mult, ALU.add
+                nc.vector.scalar_tensor_tensor(
+                    z[cb][:, tok], centred[cb][:, tok], ln_w_col[cb], rstd[:, tok], ALU.mult, ALU.mult
                 )
-            for cb in range(CB):
                 nc.tensor.matmul(
                     a_ps[t][:], w1_sb[:, cb, :], z[cb][:, tok], start=(cb == 0), stop=(cb == CB - 1)
                 )
@@ -117,7 +124,7 @@ def tile_molecularretnet_kernel(tc, base, x, ln_w, ln_b, w1, b1, w2, b2, offs, o
         h = held.tile([P, N], BF16, name="h")
         f_b2 = [held.tile([P, N], F32, name=f"f_b2_{cb}") for cb in range(CB)]
         for t, tok in enumerate(chunks):
-            nc.scalar.activation(h[:, tok], a_ps[t][:], ACT.Gelu, bias=b1_col)
+            nc.scalar.activation(h[:, tok], a_ps[t][:], ACT.Gelu, bias=a_bias[:])
             f_ps = psum.tile([P, CHUNK], F32, name="f_ps0", tag="var_f")
             nc.tensor.matmul(f_ps[:], w2_sb[:, blocks[0]], h[:, tok], start=True, stop=True)
             nc.vector.tensor_scalar(f_b2[0][:, tok], f_ps[:], b2_col[0], None, ALU.add)
@@ -128,4 +135,5 @@ def tile_molecularretnet_kernel(tc, base, x, ln_w, ln_b, w1, b1, w2, b2, offs, o
 
         for cb in range(CB):
             nc.vector.tensor_tensor(window[cb][:].indirect(offsets[:]), f_b2[cb][:], X[cb][:], ALU.add)
-            nc.sync.dma_start(out[blocks[cb], :], window[cb][:])
+            nc.sync.dma_start(out[blocks[cb], 0 : S // 2], window[cb][:, 0 : S // 2])
+            nc.scalar.dma_start(out[blocks[cb], S // 2 : S], window[cb][:, S // 2 : S])

@@ -1,5 +1,4 @@
 import concourse.mybir as mybir
-from concourse.masks import make_identity
 
 F32 = mybir.dt.float32
 BF16 = mybir.dt.bfloat16
@@ -12,8 +11,10 @@ C, F, S, N = 256, 128, 4096, 2048
 CB = C // P
 CHUNK = 512
 NCHUNK = N // CHUNK
+PIECE = 256
+NPIECE = N // PIECE
+LAG = 4
 EPS = 1e-5
-NROWS = 7
 
 FLOPS = 2 * N * C * F * 2
 
@@ -21,25 +22,28 @@ FLOPS = 2 * N * C * F * 2
 def tile_molecularretnet_kernel(tc, base, x, ln_w, ln_b, w1, b1, w2, b2, offs, out):
     nc = tc.nc
     chunks = [slice(t * CHUNK, (t + 1) * CHUNK) for t in range(NCHUNK)]
+    pieces = [slice(k * PIECE, (k + 1) * PIECE) for k in range(NPIECE)]
     blocks = [slice(cb * P, (cb + 1) * P) for cb in range(CB)]
     with (
         tc.tile_pool(name="held", bufs=1) as held,
         tc.psum_pool(name="psum", bufs=4) as psum,
     ):
         x_sb = [held.tile([P, N], F32, name=f"x_sb{cb}") for cb in range(CB)]
-        x_queue = [nc.sync, nc.scalar]
         for tok in chunks:
-            for cb in range(CB):
-                x_queue[cb].dma_start(x_sb[cb][:, tok], x[blocks[cb], tok])
+            nc.sync.dma_start(x_sb[0][:, tok], x[blocks[0], tok])
+            nc.scalar.dma_start(x_sb[1][:, tok], x[blocks[1], tok])
         w1_sb = held.tile([P, CB, F], BF16, name="w1_sb")
         nc.sync.dma_start(w1_sb[:], w1.rearrange("(b p) k -> p b k", p=P))
+        ln_w_sb = held.tile([P, CB], F32, name="ln_w_sb")
+        nc.sync.dma_start(ln_w_sb[:], ln_w.rearrange("(b p) o -> p (b o)", p=P))
+        ln_b_sb = held.tile([P, CB], F32, name="ln_b_sb")
+        nc.sync.dma_start(ln_b_sb[:], ln_b.rearrange("(b p) o -> p (b o)", p=P))
+        b1_sb = held.tile([P, 1], F32, name="b1_sb")
+        nc.sync.dma_start(b1_sb[:], b1)
+        b2_sb = held.tile([P, CB], F32, name="b2_sb")
+        nc.sync.dma_start(b2_sb[:], b2.rearrange("(b p) o -> p (b o)", p=P))
         w2_sb = held.tile([P, C], BF16, name="w2_sb")
         nc.sync.dma_start(w2_sb[:], w2)
-        rows = held.tile([NROWS, P], F32, name="rows")
-        nc.sync.dma_start(rows[0:2, :], ln_w.rearrange("(r p) o -> r (p o)", p=P))
-        nc.sync.dma_start(rows[2:4, :], ln_b.rearrange("(r p) o -> r (p o)", p=P))
-        nc.sync.dma_start(rows[4:6, :], b2.rearrange("(r p) o -> r (p o)", p=P))
-        nc.sync.dma_start(rows[6:7, :], b1.rearrange("(r p) o -> r (p o)", p=P))
         offsets = held.tile([P, N // 16], U16, name="offsets")
         nc.sync.dma_start(offsets[:], offs)
         window = [held.tile([P, S], F32, name=f"window{cb}") for cb in range(CB)]
@@ -52,87 +56,79 @@ def tile_molecularretnet_kernel(tc, base, x, ln_w, ln_b, w1, b1, w2, b2, offs, o
         nc.gpsimd.memset(avg_bf16[:], 1.0 / C)
         eps_col = held.tile([P, 1], F32, name="eps_col")
         nc.gpsimd.memset(eps_col[:], EPS)
-        identity = held.tile([NROWS, NROWS], F32, name="identity")
-        make_identity(nc, identity[:])
         warm = held.tile([P, 1], F32, name="warm")
         nc.scalar.activation(warm[:], eps_col[:], ACT.Abs_reciprocal_sqrt)
 
 
-        X = [held.tile([P, N], F32, name=f"X{cb}") for cb in range(CB)]
+        X0 = held.tile([P, N], F32, name="X0")
         both = held.tile([P, N], F32, name="both")
-        mu_ps = [psum.tile([P, CHUNK], F32, name=f"mu_ps{t}", tag="mu_a") for t in range(NCHUNK)]
-        for t, tok in enumerate(chunks):
-            nc.vector.tensor_scalar_max(X[0][:, tok], x_sb[0][:, tok], 0.0)
-            nc.scalar.activation(X[1][:, tok], x_sb[1][:, tok], ACT.Relu)
-            nc.vector.scalar_tensor_tensor(
-                both[:, tok], x_sb[1][:, tok], 0.0, X[0][:, tok], ALU.max, ALU.add
-            )
-            nc.tensor.matmul(mu_ps[t][:], avg_f32[:], both[:, tok], start=True, stop=True)
-
-        cols_ps = psum.tile([P, NROWS], F32, name="cols_ps", tag="var_f")
-        nc.tensor.matmul(cols_ps[:], rows[:], identity[:], start=True, stop=True)
-        cols = held.tile([P, NROWS], F32, name="cols")
-        nc.scalar.copy(cols[:], cols_ps[:])
-        ln_w_col = [cols[:, cb : cb + 1] for cb in range(CB)]
-        ln_b_col = [cols[:, 2 + cb : 3 + cb] for cb in range(CB)]
-        b2_col = [cols[:, 4 + cb : 5 + cb] for cb in range(CB)]
-        b1_col = cols[:, 6:7]
-
-        w1_f32 = held.tile([P, CB, F], F32, name="w1_f32")
-        nc.gpsimd.tensor_copy(w1_f32[:], w1_sb[:])
-        shift_ps = psum.tile([P, 1], F32, name="shift_ps", tag="var_f")
-        for cb in range(CB):
-            nc.tensor.matmul(
-                shift_ps[:], w1_f32[:, cb, :], ln_b_col[cb], start=(cb == 0), stop=(cb == CB - 1)
-            )
-        a_bias = held.tile([P, 1], F32, name="a_bias")
-        nc.scalar.activation(a_bias[:], shift_ps[:], ACT.Identity, bias=b1_col)
-
-        centred = [held.tile([P, N], F32, name=f"centred{cb}") for cb in range(CB)]
-        squared = [held.tile([P, N], BF16, name=f"squared{cb}") for cb in range(CB)]
-        var_ps = [psum.tile([P, CHUNK], F32, name=f"var_ps{t}", tag="var_f") for t in range(NCHUNK)]
+        centred = [held.tile([P, N], BF16, name=f"centred{cb}") for cb in range(CB)]
+        squared = held.tile([P, CB, N], BF16, name="squared", tag="squared_scaled")
         rstd = held.tile([P, N], F32, name="rstd")
-        for t in range(NCHUNK + 1):
-            if t < NCHUNK:
-                tok = chunks[t]
-                nc.vector.tensor_tensor(centred[0][:, tok], X[0][:, tok], mu_ps[t][:], ALU.subtract)
+        mu_ps = {}
+        for step in range(NPIECE + LAG):
+            if step < NPIECE:
+                tok = pieces[step]
+                nc.scalar.activation(X0[:, tok], x_sb[0][:, tok], ACT.Relu)
                 nc.vector.scalar_tensor_tensor(
-                    centred[1][:, tok], x_sb[1][:, tok], 0.0, mu_ps[t][:], ALU.max, ALU.subtract
+                    both[:, tok], x_sb[1][:, tok], 0.0, X0[:, tok], ALU.max, ALU.add
                 )
-                nc.gpsimd.tensor_tensor(squared[0][:, tok], centred[0][:, tok], centred[0][:, tok], ALU.mult)
-                nc.scalar.activation(squared[1][:, tok], centred[1][:, tok], ACT.Square)
+                mu_ps[step] = psum.tile([P, PIECE], F32, name=f"mu_ps{step}", tag="mu_a")
+                nc.tensor.matmul(mu_ps[step][:], avg_f32[:], both[:, tok], start=True, stop=True)
+            if step == NPIECE - 1:
+                w1_ln = held.tile([P, CB, F], BF16, name="w1_ln")
+                for cb in range(CB):
+                    nc.gpsimd.tensor_scalar_mul(w1_ln[:, cb, :], w1_sb[:, cb, :], ln_w_sb[:, cb : cb + 1])
+                w1_f32 = held.tile([P, CB, F], F32, name="w1_f32")
+                nc.gpsimd.tensor_copy(w1_f32[:], w1_sb[:])
+                shift_ps = psum.tile([P, 1], F32, name="shift_ps", tag="var_f")
                 for cb in range(CB):
                     nc.tensor.matmul(
-                        var_ps[t][:], avg_bf16[:], squared[cb][:, tok], start=(cb == 0), stop=(cb == CB - 1)
+                        shift_ps[:], w1_f32[:, cb, :], ln_b_sb[:, cb : cb + 1], start=(cb == 0), stop=(cb == CB - 1)
                     )
-            if t > 0:
-                nc.scalar.activation(
-                    rstd[:, chunks[t - 1]], var_ps[t - 1][:], ACT.Abs_reciprocal_sqrt, bias=eps_col[:]
-                )
-
-        z = [held.tile([P, N], BF16, name=f"z{cb}") for cb in range(CB)]
-        a_ps = [psum.tile([P, CHUNK], F32, name=f"a_ps{t}", tag="mu_a") for t in range(NCHUNK)]
-        for t, tok in enumerate(chunks):
-            for cb in range(CB):
+                a_bias = held.tile([P, 1], F32, name="a_bias")
+                nc.vector.tensor_tensor(a_bias[:], shift_ps[:], b1_sb[:], ALU.add)
+            if step >= LAG:
+                k = step - LAG
+                tok = pieces[k]
+                nc.vector.tensor_tensor(centred[0][:, tok], X0[:, tok], mu_ps[k][:], ALU.subtract)
                 nc.vector.scalar_tensor_tensor(
-                    z[cb][:, tok], centred[cb][:, tok], ln_w_col[cb], rstd[:, tok], ALU.mult, ALU.mult
+                    centred[1][:, tok], x_sb[1][:, tok], 0.0, mu_ps[k][:], ALU.max, ALU.subtract
                 )
+                nc.vector.tensor_tensor(squared[:, 0, tok], centred[0][:, tok], centred[0][:, tok], ALU.mult)
+                nc.scalar.activation(squared[:, 1, tok], centred[1][:, tok], ACT.Square)
+                var_ps = psum.tile([P, PIECE], F32, name=f"var_ps{k}", tag="var_f")
+                for cb in range(CB):
+                    nc.tensor.matmul(
+                        var_ps[:], avg_bf16[:], squared[:, cb, tok], start=(cb == 0), stop=(cb == CB - 1)
+                    )
+                nc.scalar.activation(rstd[:, tok], var_ps[:], ACT.Abs_reciprocal_sqrt, bias=eps_col[:])
+
+        a_ps = []
+        for t, tok in enumerate(chunks):
+            a_ps.append(psum.tile([P, CHUNK], F32, name=f"a_ps{t}", tag="mu_a"))
+            for cb in range(CB):
                 nc.tensor.matmul(
-                    a_ps[t][:], w1_sb[:, cb, :], z[cb][:, tok], start=(cb == 0), stop=(cb == CB - 1)
+                    a_ps[t][:], w1_ln[:, cb, :], centred[cb][:, tok], start=(cb == 0), stop=(cb == CB - 1)
                 )
 
+        scaled = held.tile([P, N], F32, name="scaled", tag="squared_scaled")
         h = held.tile([P, N], BF16, name="h")
         f_b2 = [held.tile([P, N], F32, name=f"f_b2_{cb}") for cb in range(CB)]
         for t, tok in enumerate(chunks):
-            nc.scalar.activation(h[:, tok], a_ps[t][:], ACT.Gelu, bias=a_bias[:])
+            nc.vector.tensor_tensor(scaled[:, tok], a_ps[t][:], rstd[:, tok], ALU.mult)
+            nc.scalar.activation(h[:, tok], scaled[:, tok], ACT.Gelu, bias=a_bias[:])
             f_ps = psum.tile([P, CHUNK], F32, name="f_ps0", tag="var_f")
             nc.tensor.matmul(f_ps[:], w2_sb[:, blocks[0]], h[:, tok], start=True, stop=True)
-            nc.vector.tensor_scalar(f_b2[0][:, tok], f_ps[:], b2_col[0], None, ALU.add)
+            nc.vector.tensor_scalar(f_b2[0][:, tok], f_ps[:], b2_sb[:, 0:1], None, ALU.add)
+        X1 = held.tile([P, N], F32, name="X1", tag="squared_scaled")
         for tok in chunks:
+            nc.scalar.activation(X1[:, tok], x_sb[1][:, tok], ACT.Relu)
             f_ps = psum.tile([P, CHUNK], F32, name="f_ps1", tag="var_f")
             nc.tensor.matmul(f_ps[:], w2_sb[:, blocks[1]], h[:, tok], start=True, stop=True)
-            nc.scalar.activation(f_b2[1][:, tok], f_ps[:], ACT.Identity, bias=b2_col[1])
+            nc.scalar.activation(f_b2[1][:, tok], f_ps[:], ACT.Identity, bias=b2_sb[:, 1:2])
 
+        X = [X0, X1]
         for cb in range(CB):
             nc.vector.tensor_tensor(window[cb][:].indirect(offsets[:]), f_b2[cb][:], X[cb][:], ALU.add)
             nc.sync.dma_start(out[blocks[cb], 0 : S // 2], window[cb][:, 0 : S // 2])

@@ -86,8 +86,6 @@ def tile_molecularretnet_kernel(tc, base, x, ln_w, ln_b, w1, b1, w2, b2, offs, o
                     nc.tensor.matmul(
                         shift_ps[:], w1_f32[:, cb, :], ln_b_sb[:, cb : cb + 1], start=(cb == 0), stop=(cb == CB - 1)
                     )
-                a_bias = held.tile([P, 1], F32, name="a_bias")
-                nc.vector.tensor_tensor(a_bias[:], shift_ps[:], b1_sb[:], ALU.add)
             if step >= LAG:
                 k = step - LAG
                 tok = pieces[k]
@@ -104,6 +102,9 @@ def tile_molecularretnet_kernel(tc, base, x, ln_w, ln_b, w1, b1, w2, b2, offs, o
                     )
                 nc.scalar.activation(rstd[:, tok], var_ps[:], ACT.Abs_reciprocal_sqrt, bias=eps_col[:])
 
+        a_bias = held.tile([P, 1], F32, name="a_bias")
+        nc.vector.tensor_tensor(a_bias[:], shift_ps[:], b1_sb[:], ALU.add)
+
         a_ps = []
         for t, tok in enumerate(chunks):
             a_ps.append(psum.tile([P, CHUNK], F32, name=f"a_ps{t}", tag="mu_a"))
@@ -115,10 +116,11 @@ def tile_molecularretnet_kernel(tc, base, x, ln_w, ln_b, w1, b1, w2, b2, offs, o
         scaled = held.tile([P, N], F32, name="scaled", tag="squared_scaled")
         h = held.tile([P, N], BF16, name="h")
         f_b2 = [held.tile([P, N], F32, name=f"f_b2_{cb}") for cb in range(CB)]
-        for t, tok in enumerate(chunks):
-            nc.vector.tensor_tensor(scaled[:, tok], a_ps[t][:], rstd[:, tok], ALU.mult)
+        for k, tok in enumerate(pieces):
+            half = slice((k % 2) * PIECE, (k % 2 + 1) * PIECE)
+            nc.vector.tensor_tensor(scaled[:, tok], a_ps[k // 2][:, half], rstd[:, tok], ALU.mult)
             nc.scalar.activation(h[:, tok], scaled[:, tok], ACT.Gelu, bias=a_bias[:])
-            f_ps = psum.tile([P, CHUNK], F32, name="f_ps0", tag="var_f")
+            f_ps = psum.tile([P, PIECE], F32, name="f_ps0", tag="var_f")
             nc.tensor.matmul(f_ps[:], w2_sb[:, blocks[0]], h[:, tok], start=True, stop=True)
             nc.vector.tensor_scalar(f_b2[0][:, tok], f_ps[:], b2_sb[:, 0:1], None, ALU.add)
         X1 = held.tile([P, N], F32, name="X1", tag="squared_scaled")

@@ -13,6 +13,7 @@ CHUNK = 512
 NCHUNK = N // CHUNK
 PIECE = 256
 NPIECE = N // PIECE
+VECTOR_SQUARES = 2
 LAG = 4
 EPS = 1e-5
 
@@ -93,8 +94,11 @@ def tile_molecularretnet_kernel(tc, base, x, ln_w, ln_b, w1, b1, w2, b2, offs, o
                 nc.vector.scalar_tensor_tensor(
                     centred[1][:, tok], x_sb[1][:, tok], 0.0, mu_ps[k][:], ALU.max, ALU.subtract
                 )
-                nc.vector.tensor_tensor(squared[:, 0, tok], centred[0][:, tok], centred[0][:, tok], ALU.mult)
-                nc.scalar.activation(squared[:, 1, tok], centred[1][:, tok], ACT.Square)
+                for cb in range(CB):
+                    if k < NPIECE - VECTOR_SQUARES:
+                        nc.scalar.activation(squared[:, cb, tok], centred[cb][:, tok], ACT.Square)
+                    else:
+                        nc.vector.tensor_tensor(squared[:, cb, tok], centred[cb][:, tok], centred[cb][:, tok], ALU.mult)
                 var_ps = psum.tile([P, PIECE], F32, name=f"var_ps{k}", tag="var_f")
                 for cb in range(CB):
                     nc.tensor.matmul(

@@ -30,9 +30,12 @@ def tile_molecularretnet_kernel(tc, base, x, ln_w, ln_b, w1, b1, w2, b2, offs, o
         tc.psum_pool(name="psum", bufs=4) as psum,
     ):
         x_sb = [held.tile([P, N], F32, name=f"x_sb{cb}") for cb in range(CB)]
-        for tok in chunks:
+        x_loads = pieces[:2] + chunks[1:]
+        for tok in x_loads:
             nc.sync.dma_start(x_sb[0][:, tok], x[blocks[0], tok])
-            nc.scalar.dma_start(x_sb[1][:, tok], x[blocks[1], tok])
+            if tok != x_loads[-1]:
+                nc.scalar.dma_start(x_sb[1][:, tok], x[blocks[1], tok])
+        nc.sync.dma_start(x_sb[1][:, x_loads[-1]], x[blocks[1], x_loads[-1]])
         w1_sb = held.tile([P, CB, F], BF16, name="w1_sb")
         nc.sync.dma_start(w1_sb[:], w1.rearrange("(b p) k -> p b k", p=P))
         ln_w_sb = held.tile([P, CB], F32, name="ln_w_sb")
@@ -70,7 +73,10 @@ def tile_molecularretnet_kernel(tc, base, x, ln_w, ln_b, w1, b1, w2, b2, offs, o
         for step in range(NPIECE + LAG):
             if step < NPIECE:
                 tok = pieces[step]
-                nc.scalar.activation(X0[:, tok], x_sb[0][:, tok], ACT.Relu)
+                if tok.stop <= CHUNK:
+                    nc.vector.tensor_scalar_max(X0[:, tok], x_sb[0][:, tok], 0.0)
+                else:
+                    nc.scalar.activation(X0[:, tok], x_sb[0][:, tok], ACT.Relu)
                 nc.vector.scalar_tensor_tensor(
                     both[:, tok], x_sb[1][:, tok], 0.0, X0[:, tok], ALU.max, ALU.add
                 )

@@ -30,12 +30,12 @@ def tile_molecularretnet_kernel(tc, base, x, ln_w, ln_b, w1, b1, w2, b2, offs, o
         tc.psum_pool(name="psum", bufs=4) as psum,
     ):
         x_sb = [held.tile([P, N], F32, name=f"x_sb{cb}") for cb in range(CB)]
-        x_loads = pieces[:2] + chunks[1:]
-        for tok in x_loads:
+        for tok in pieces[:2] + chunks[1:]:
             nc.sync.dma_start(x_sb[0][:, tok], x[blocks[0], tok])
-            if tok != x_loads[-1]:
+            if tok.start < N // 2:
                 nc.scalar.dma_start(x_sb[1][:, tok], x[blocks[1], tok])
-        nc.sync.dma_start(x_sb[1][:, x_loads[-1]], x[blocks[1], x_loads[-1]])
+            else:
+                nc.sync.dma_start(x_sb[1][:, tok], x[blocks[1], tok])
         w1_sb = held.tile([P, CB, F], BF16, name="w1_sb")
         nc.sync.dma_start(w1_sb[:], w1.rearrange("(b p) k -> p b k", p=P))
         ln_w_sb = held.tile([P, CB], F32, name="ln_w_sb")

@@ -1,4 +1,5 @@
 import concourse.mybir as mybir
+from concourse.masks import make_identity
 
 F32 = mybir.dt.float32
 BF16 = mybir.dt.bfloat16
@@ -13,8 +14,7 @@ CHUNK = 512
 NCHUNK = N // CHUNK
 PIECE = 256
 NPIECE = N // PIECE
-VECTOR_SQUARES = 2
-LAG = 4
+TB = CHUNK // P
 EPS = 1e-5
 
 FLOPS = 2 * N * C * F * 2
@@ -22,27 +22,27 @@ FLOPS = 2 * N * C * F * 2
 
 def tile_molecularretnet_kernel(tc, base, x, ln_w, ln_b, w1, b1, w2, b2, offs, out):
     nc = tc.nc
-    chunks = [slice(t * CHUNK, (t + 1) * CHUNK) for t in range(NCHUNK)]
-    pieces = [slice(k * PIECE, (k + 1) * PIECE) for k in range(NPIECE)]
+    chunks = [slice(t, t + CHUNK) for t in range(0, N, CHUNK)]
+    pieces = [slice(t, t + PIECE) for t in range(0, N, PIECE)]
+    loads = pieces[:2] + chunks[1:]
     blocks = [slice(cb * P, (cb + 1) * P) for cb in range(CB)]
     with (
         tc.tile_pool(name="held", bufs=1) as held,
-        tc.psum_pool(name="psum", bufs=4) as psum,
+        tc.tile_pool(name="small", bufs=2) as small,
+        tc.psum_pool(name="psum", bufs=8) as psum,
     ):
         x_sb = [held.tile([P, N], F32, name=f"x_sb{cb}") for cb in range(CB)]
-        for tok in pieces[:2] + chunks[1:]:
-            nc.sync.dma_start(x_sb[0][:, tok], x[blocks[0], tok])
-            if tok.start < N // 2:
-                nc.scalar.dma_start(x_sb[1][:, tok], x[blocks[1], tok])
-            else:
-                nc.sync.dma_start(x_sb[1][:, tok], x[blocks[1], tok])
         w1_sb = held.tile([P, CB, F], BF16, name="w1_sb")
-        nc.sync.dma_start(w1_sb[:], w1.rearrange("(b p) k -> p b k", p=P))
         ln_w_sb = held.tile([P, CB], F32, name="ln_w_sb")
-        nc.sync.dma_start(ln_w_sb[:], ln_w.rearrange("(b p) o -> p (b o)", p=P))
+        nc.scalar.dma_start(w1_sb[:], w1.rearrange("(b p) k -> p b k", p=P))
+        nc.scalar.dma_start(ln_w_sb[:], ln_w.rearrange("(b p) o -> p (b o)", p=P))
         ln_b_sb = held.tile([P, CB], F32, name="ln_b_sb")
-        nc.sync.dma_start(ln_b_sb[:], ln_b.rearrange("(b p) o -> p (b o)", p=P))
         b1_sb = held.tile([P, 1], F32, name="b1_sb")
+        for tok in loads:
+            nc.sync.dma_start(x_sb[0][:, tok], x[blocks[0], tok])
+        for tok in loads:
+            nc.sync.dma_start(x_sb[1][:, tok], x[blocks[1], tok])
+        nc.sync.dma_start(ln_b_sb[:], ln_b.rearrange("(b p) o -> p (b o)", p=P))
         nc.sync.dma_start(b1_sb[:], b1)
         b2_sb = held.tile([P, CB], F32, name="b2_sb")
         nc.sync.dma_start(b2_sb[:], b2.rearrange("(b p) o -> p (b o)", p=P))
@@ -54,89 +54,108 @@ def tile_molecularretnet_kernel(tc, base, x, ln_w, ln_b, w1, b1, w2, b2, offs, o
         for cb in range(CB):
             nc.sync.dma_start(window[cb][:], base[blocks[cb], :])
 
-        avg_f32 = held.tile([P, P], F32, name="avg_f32")
-        nc.gpsimd.memset(avg_f32[:], 1.0 / C)
-        avg_bf16 = held.tile([P, P], BF16, name="avg_bf16")
-        nc.gpsimd.memset(avg_bf16[:], 1.0 / C)
+        avg0 = held.tile([P, P], BF16, name="avg0")
+        nc.gpsimd.memset(avg0[:], 1.0 / P)
+        avg = held.tile([P, P], BF16, name="avg")
+        nc.gpsimd.memset(avg[:], 1.0 / C)
         eps_col = held.tile([P, 1], F32, name="eps_col")
         nc.gpsimd.memset(eps_col[:], EPS)
+        ident = held.tile([P, P], F32, name="ident")
+        make_identity(nc, ident[:])
         warm = held.tile([P, 1], F32, name="warm")
         nc.scalar.activation(warm[:], eps_col[:], ACT.Abs_reciprocal_sqrt)
 
-
+        d = [held.tile([P, N], BF16, name=f"d{cb}") for cb in range(CB)]
+        xb0 = held.tile([P, N], BF16, name="xb0", tag="xb0_squared0")
+        squared = [
+            held.tile([P, N], BF16, name="squared0", tag="xb0_squared0"),
+            held.tile([P, N], BF16, name="squared1"),
+        ]
         X0 = held.tile([P, N], F32, name="X0")
-        both = held.tile([P, N], F32, name="both")
-        centred = [held.tile([P, N], BF16, name=f"centred{cb}") for cb in range(CB)]
-        squared = held.tile([P, CB, N], BF16, name="squared", tag="squared_scaled")
-        rstd = held.tile([P, N], F32, name="rstd")
-        mu_ps = {}
-        for step in range(NPIECE + LAG):
-            if step < NPIECE:
-                tok = pieces[step]
-                if tok.stop <= CHUNK:
-                    nc.vector.tensor_scalar_max(X0[:, tok], x_sb[0][:, tok], 0.0)
-                else:
-                    nc.scalar.activation(X0[:, tok], x_sb[0][:, tok], ACT.Relu)
-                nc.vector.scalar_tensor_tensor(
-                    both[:, tok], x_sb[1][:, tok], 0.0, X0[:, tok], ALU.max, ALU.add
-                )
-                mu_ps[step] = psum.tile([P, PIECE], F32, name=f"mu_ps{step}", tag="mu_a")
-                nc.tensor.matmul(mu_ps[step][:], avg_f32[:], both[:, tok], start=True, stop=True)
-            if step == NPIECE - 1:
-                w1_ln = held.tile([P, CB, F], BF16, name="w1_ln")
-                for cb in range(CB):
-                    nc.gpsimd.tensor_scalar_mul(w1_ln[:, cb, :], w1_sb[:, cb, :], ln_w_sb[:, cb : cb + 1])
-                w1_f32 = held.tile([P, CB, F], F32, name="w1_f32")
-                nc.gpsimd.tensor_copy(w1_f32[:], w1_sb[:])
-                shift_ps = psum.tile([P, 1], F32, name="shift_ps", tag="var_f")
-                for cb in range(CB):
-                    nc.tensor.matmul(
-                        shift_ps[:], w1_f32[:, cb, :], ln_b_sb[:, cb : cb + 1], start=(cb == 0), stop=(cb == CB - 1)
-                    )
-            if step >= LAG:
-                k = step - LAG
-                tok = pieces[k]
-                nc.vector.tensor_tensor(centred[0][:, tok], X0[:, tok], mu_ps[k][:], ALU.subtract)
-                nc.vector.scalar_tensor_tensor(
-                    centred[1][:, tok], x_sb[1][:, tok], 0.0, mu_ps[k][:], ALU.max, ALU.subtract
-                )
-                for cb in range(CB):
-                    if k < NPIECE - VECTOR_SQUARES:
-                        nc.scalar.activation(squared[:, cb, tok], centred[cb][:, tok], ACT.Square)
-                    else:
-                        nc.vector.tensor_tensor(squared[:, cb, tok], centred[cb][:, tok], centred[cb][:, tok], ALU.mult)
-                var_ps = psum.tile([P, PIECE], F32, name=f"var_ps{k}", tag="var_f")
-                for cb in range(CB):
-                    nc.tensor.matmul(
-                        var_ps[:], avg_bf16[:], squared[:, cb, tok], start=(cb == 0), stop=(cb == CB - 1)
-                    )
-                nc.scalar.activation(rstd[:, tok], var_ps[:], ACT.Abs_reciprocal_sqrt, bias=eps_col[:])
-
-        a_bias = held.tile([P, 1], F32, name="a_bias")
-        nc.vector.tensor_tensor(a_bias[:], shift_ps[:], b1_sb[:], ALU.add)
-
-        a_ps = []
-        for t, tok in enumerate(chunks):
-            a_ps.append(psum.tile([P, CHUNK], F32, name=f"a_ps{t}", tag="mu_a"))
-            for cb in range(CB):
-                nc.tensor.matmul(
-                    a_ps[t][:], w1_ln[:, cb, :], centred[cb][:, tok], start=(cb == 0), stop=(cb == CB - 1)
-                )
-
-        scaled = held.tile([P, N], F32, name="scaled", tag="squared_scaled")
-        h = held.tile([P, N], BF16, name="h")
+        aT_scaled = held.tile([P, N // P, F], F32, name="aT_scaled", tag="aT_scaled_X1")
+        rstd = held.tile([P, N // P], F32, name="rstd")
+        var = held.tile([P, N // P], F32, name="var", tag="var_h")
         f_b2 = [held.tile([P, N], F32, name=f"f_b2_{cb}") for cb in range(CB)]
+        a_bias = held.tile([P, 1], F32, name="a_bias")
+
+        s_ps, aT_ps = {}, {}
+        weights = held.tile([P, CB, F], BF16, name="weights")
+        w1_ln = held.tile([P, CB, F], BF16, name="w1_ln")
+        for cb in range(CB):
+            nc.vector.tensor_scalar_mul(w1_ln[:, cb, :], w1_sb[:, cb, :], ln_w_sb[:, cb : cb + 1])
+        mean_w = psum.tile([P, F], F32, name="mean_w", tag="bank")
+        for cb in range(CB):
+            nc.tensor.matmul(mean_w[:], avg[:], w1_ln[:, cb, :], start=(cb == 0), stop=(cb == CB - 1))
+        for cb in range(CB):
+            nc.vector.scalar_tensor_tensor(
+                weights[:, cb, :], w1_sb[:, cb, :], ln_w_sb[:, cb : cb + 1], mean_w[:], ALU.mult, ALU.subtract
+            )
+        w1_f32 = held.tile([P, CB, F], F32, name="w1_f32")
+        nc.gpsimd.tensor_copy(w1_f32[:], w1_sb[:])
+        for i, tok in enumerate(loads):
+            nc.scalar.activation(xb0[:, tok], x_sb[0][:, tok], ACT.Relu)
+            s_ps[i] = psum.tile([P, tok.stop - tok.start], F32, name=f"s_ps{i}", tag="bank")
+            nc.tensor.matmul(s_ps[i][:], avg0[:], xb0[:, tok], start=True, stop=True)
+        bias_ps = psum.tile([P, 1], F32, name="bias_ps", tag="bank")
+        for cb in range(CB):
+            nc.tensor.matmul(
+                bias_ps[:], w1_f32[:, cb, :], ln_b_sb[:, cb : cb + 1], start=(cb == 0), stop=(cb == CB - 1)
+            )
+        nc.vector.tensor_tensor(a_bias[:], bias_ps[:], b1_sb[:], ALU.add)
+        for i, tok in enumerate(loads):
+            for cb in range(CB):
+                nc.vector.scalar_tensor_tensor(
+                    d[cb][:, tok], x_sb[cb][:, tok], 0.0, s_ps[i][:], ALU.max, ALU.subtract
+                )
+            nc.scalar.activation(squared[0][:, tok], d[0][:, tok], ACT.Square)
+            nc.vector.tensor_tensor(squared[1][:, tok], d[1][:, tok], d[1][:, tok], ALU.mult)
+        for c in range(NCHUNK):
+            Ed = psum.tile([P, TB], F32, name=f"Ed{c}", tag="bank")
+            Ed2 = small.tile([P, TB], F32, name=f"Ed2_{c}", tag="Ed2")
+            d2 = psum.tile([P, TB], F32, name=f"d2_{c}", tag="bank")
+            for j in range(TB):
+                tb = slice((c * TB + j) * P, (c * TB + j + 1) * P)
+                for cb in range(CB):
+                    nc.tensor.matmul(
+                        Ed[:, j : j + 1], d[cb][:, tb], avg[:, 0:1], start=(cb == 0), stop=(cb == CB - 1)
+                    )
+            nc.scalar.activation(Ed2[:], Ed[:], ACT.Square)
+            for j in range(TB):
+                tb = slice((c * TB + j) * P, (c * TB + j + 1) * P)
+                for cb in range(CB):
+                    nc.tensor.matmul(
+                        d2[:, j : j + 1], squared[cb][:, tb], avg[:, 0:1], start=(cb == 0), stop=(cb == CB - 1)
+                    )
+            cols = slice(c * TB, (c + 1) * TB)
+            nc.vector.tensor_tensor(var[:, cols], d2[:], Ed2[:], ALU.subtract)
+            nc.scalar.activation(rstd[:, cols], var[:, cols], ACT.Abs_reciprocal_sqrt, bias=eps_col[:])
+        nc.scalar.activation(warm[:], rstd[:, N // P - 1 :], ACT.Gelu)
+        for c in range(NCHUNK):
+            aT_ps[c] = psum.tile([P, TB, F], F32, name=f"aT_ps{c}", tag="bank")
+            for j in range(TB):
+                tb = slice((c * TB + j) * P, (c * TB + j + 1) * P)
+                for cb in range(CB):
+                    nc.tensor.matmul(
+                        aT_ps[c][:, j, :], d[cb][:, tb], weights[:, cb, :], start=(cb == 0), stop=(cb == CB - 1)
+                    )
+        h = held.tile([P, N], BF16, name="h", tag="var_h")
+        a_ps = [psum.tile([P, CHUNK], F32, name=f"a_ps{c}", tag="bank") for c in range(NCHUNK)]
+        for c in range(NCHUNK):
+            for j in range(TB):
+                jj = c * TB + j
+                nc.vector.tensor_scalar_mul(aT_scaled[:, jj, :], aT_ps[c][:, j, :], rstd[:, jj : jj + 1])
+                nc.tensor.transpose(a_ps[c][:, j * P : (j + 1) * P], aT_scaled[:, jj, :], ident[:])
         for k, tok in enumerate(pieces):
-            half = slice((k % 2) * PIECE, (k % 2 + 1) * PIECE)
-            nc.vector.tensor_tensor(scaled[:, tok], a_ps[k // 2][:, half], rstd[:, tok], ALU.mult)
-            nc.scalar.activation(h[:, tok], scaled[:, tok], ACT.Gelu, bias=a_bias[:])
-            f_ps = psum.tile([P, PIECE], F32, name="f_ps0", tag="var_f")
+            in_chunk = slice(k * PIECE % CHUNK, k * PIECE % CHUNK + PIECE)
+            nc.scalar.activation(h[:, tok], a_ps[k * PIECE // CHUNK][:, in_chunk], ACT.Gelu, bias=a_bias[:])
+            f_ps = psum.tile([P, PIECE], F32, name="f_ps0", tag="bank")
             nc.tensor.matmul(f_ps[:], w2_sb[:, blocks[0]], h[:, tok], start=True, stop=True)
             nc.vector.tensor_scalar(f_b2[0][:, tok], f_ps[:], b2_sb[:, 0:1], None, ALU.add)
-        X1 = held.tile([P, N], F32, name="X1", tag="squared_scaled")
+            nc.scalar.activation(X0[:, tok], x_sb[0][:, tok], ACT.Relu)
+        X1 = held.tile([P, N], F32, name="X1", tag="aT_scaled_X1")
         for tok in chunks:
             nc.scalar.activation(X1[:, tok], x_sb[1][:, tok], ACT.Relu)
-            f_ps = psum.tile([P, CHUNK], F32, name="f_ps1", tag="var_f")
+            f_ps = psum.tile([P, CHUNK], F32, name="f_ps1", tag="bank")
             nc.tensor.matmul(f_ps[:], w2_sb[:, blocks[1]], h[:, tok], start=True, stop=True)
             nc.scalar.activation(f_b2[1][:, tok], f_ps[:], ACT.Identity, bias=b2_sb[:, 1:2])
 

@@ -15,6 +15,7 @@ NCHUNK = N // CHUNK
 PIECE = 256
 NPIECE = N // PIECE
 TB = CHUNK // P
+LEAD = 2
 EPS = 1e-5
 
 FLOPS = 2 * N * C * F * 2
@@ -34,14 +35,15 @@ def tile_molecularretnet_kernel(tc, base, x, ln_w, ln_b, w1, b1, w2, b2, offs, o
         x_sb = [held.tile([P, N], F32, name=f"x_sb{cb}") for cb in range(CB)]
         w1_sb = held.tile([P, CB, F], BF16, name="w1_sb")
         ln_w_sb = held.tile([P, CB], F32, name="ln_w_sb")
-        nc.scalar.dma_start(w1_sb[:], w1.rearrange("(b p) k -> p b k", p=P))
         nc.scalar.dma_start(ln_w_sb[:], ln_w.rearrange("(b p) o -> p (b o)", p=P))
+        nc.scalar.dma_start(w1_sb[:], w1.rearrange("(b p) k -> p b k", p=P))
         ln_b_sb = held.tile([P, CB], F32, name="ln_b_sb")
         b1_sb = held.tile([P, 1], F32, name="b1_sb")
-        for tok in loads:
-            nc.sync.dma_start(x_sb[0][:, tok], x[blocks[0], tok])
-        for tok in loads:
-            nc.sync.dma_start(x_sb[1][:, tok], x[blocks[1], tok])
+        for step in range(len(loads) + LEAD):
+            if step < len(loads):
+                nc.sync.dma_start(x_sb[0][:, loads[step]], x[blocks[0], loads[step]])
+            if step >= LEAD:
+                nc.sync.dma_start(x_sb[1][:, loads[step - LEAD]], x[blocks[1], loads[step - LEAD]])
         nc.sync.dma_start(ln_b_sb[:], ln_b.rearrange("(b p) o -> p (b o)", p=P))
         nc.sync.dma_start(b1_sb[:], b1)
         b2_sb = held.tile([P, CB], F32, name="b2_sb")
@@ -79,6 +81,10 @@ def tile_molecularretnet_kernel(tc, base, x, ln_w, ln_b, w1, b1, w2, b2, offs, o
         a_bias = held.tile([P, 1], F32, name="a_bias")
 
         s_ps, aT_ps = {}, {}
+        for i, tok in enumerate(loads):
+            nc.scalar.activation(xb0[:, tok], x_sb[0][:, tok], ACT.Relu)
+            s_ps[i] = psum.tile([P, tok.stop - tok.start], F32, name=f"s_ps{i}", tag="bank")
+            nc.tensor.matmul(s_ps[i][:], avg0[:], xb0[:, tok], start=True, stop=True)
         weights = held.tile([P, CB, F], BF16, name="weights")
         w1_ln = held.tile([P, CB, F], BF16, name="w1_ln")
         for cb in range(CB):
@@ -93,51 +99,50 @@ def tile_molecularretnet_kernel(tc, base, x, ln_w, ln_b, w1, b1, w2, b2, offs, o
         w1_f32 = held.tile([P, CB, F], F32, name="w1_f32")
         nc.gpsimd.tensor_copy(w1_f32[:], w1_sb[:])
         for i, tok in enumerate(loads):
-            nc.scalar.activation(xb0[:, tok], x_sb[0][:, tok], ACT.Relu)
-            s_ps[i] = psum.tile([P, tok.stop - tok.start], F32, name=f"s_ps{i}", tag="bank")
-            nc.tensor.matmul(s_ps[i][:], avg0[:], xb0[:, tok], start=True, stop=True)
-        bias_ps = psum.tile([P, 1], F32, name="bias_ps", tag="bank")
-        for cb in range(CB):
-            nc.tensor.matmul(
-                bias_ps[:], w1_f32[:, cb, :], ln_b_sb[:, cb : cb + 1], start=(cb == 0), stop=(cb == CB - 1)
-            )
-        nc.vector.tensor_tensor(a_bias[:], bias_ps[:], b1_sb[:], ALU.add)
-        for i, tok in enumerate(loads):
             for cb in range(CB):
                 nc.vector.scalar_tensor_tensor(
                     d[cb][:, tok], x_sb[cb][:, tok], 0.0, s_ps[i][:], ALU.max, ALU.subtract
                 )
             nc.scalar.activation(squared[0][:, tok], d[0][:, tok], ACT.Square)
             nc.vector.tensor_tensor(squared[1][:, tok], d[1][:, tok], d[1][:, tok], ALU.mult)
-        for c in range(NCHUNK):
-            Ed = psum.tile([P, TB], F32, name=f"Ed{c}", tag="bank")
-            Ed2 = small.tile([P, TB], F32, name=f"Ed2_{c}", tag="Ed2")
-            d2 = psum.tile([P, TB], F32, name=f"d2_{c}", tag="bank")
-            for j in range(TB):
-                tb = slice((c * TB + j) * P, (c * TB + j + 1) * P)
-                for cb in range(CB):
-                    nc.tensor.matmul(
-                        Ed[:, j : j + 1], d[cb][:, tb], avg[:, 0:1], start=(cb == 0), stop=(cb == CB - 1)
-                    )
-            nc.scalar.activation(Ed2[:], Ed[:], ACT.Square)
-            for j in range(TB):
-                tb = slice((c * TB + j) * P, (c * TB + j + 1) * P)
-                for cb in range(CB):
-                    nc.tensor.matmul(
-                        d2[:, j : j + 1], squared[cb][:, tb], avg[:, 0:1], start=(cb == 0), stop=(cb == CB - 1)
-                    )
-            cols = slice(c * TB, (c + 1) * TB)
-            nc.vector.tensor_tensor(var[:, cols], d2[:], Ed2[:], ALU.subtract)
-            nc.scalar.activation(rstd[:, cols], var[:, cols], ACT.Abs_reciprocal_sqrt, bias=eps_col[:])
+        for step in range(NCHUNK + 1):
+            if step < NCHUNK:
+                c = step
+                Ed = psum.tile([P, TB], F32, name=f"Ed{c}", tag="bank")
+                Ed2 = small.tile([P, TB], F32, name=f"Ed2_{c}", tag="Ed2")
+                d2 = psum.tile([P, TB], F32, name=f"d2_{c}", tag="bank")
+                for j in range(TB):
+                    tb = slice((c * TB + j) * P, (c * TB + j + 1) * P)
+                    for cb in range(CB):
+                        nc.tensor.matmul(
+                            Ed[:, j : j + 1], d[cb][:, tb], avg[:, 0:1], start=(cb == 0), stop=(cb == CB - 1)
+                        )
+                nc.scalar.activation(Ed2[:], Ed[:], ACT.Square)
+                for j in range(TB):
+                    tb = slice((c * TB + j) * P, (c * TB + j + 1) * P)
+                    for cb in range(CB):
+                        nc.tensor.matmul(
+                            d2[:, j : j + 1], squared[cb][:, tb], avg[:, 0:1], start=(cb == 0), stop=(cb == CB - 1)
+                        )
+                cols = slice(c * TB, (c + 1) * TB)
+                nc.vector.tensor_tensor(var[:, cols], d2[:], Ed2[:], ALU.subtract)
+                nc.scalar.activation(rstd[:, cols], var[:, cols], ACT.Abs_reciprocal_sqrt, bias=eps_col[:])
+            if step > 0:
+                c = step - 1
+                aT_ps[c] = psum.tile([P, TB, F], F32, name=f"aT_ps{c}", tag="bank")
+                for j in range(TB):
+                    tb = slice((c * TB + j) * P, (c * TB + j + 1) * P)
+                    for cb in range(CB):
+                        nc.tensor.matmul(
+                            aT_ps[c][:, j, :], d[cb][:, tb], weights[:, cb, :], start=(cb == 0), stop=(cb == CB - 1)
+                        )
+        bias_ps = psum.tile([P, 1], F32, name="bias_ps", tag="bank")
+        for cb in range(CB):
+            nc.tensor.matmul(
+                bias_ps[:], w1_f32[:, cb, :], ln_b_sb[:, cb : cb + 1], start=(cb == 0), stop=(cb == CB - 1)
+            )
+        nc.vector.tensor_tensor(a_bias[:], bias_ps[:], b1_sb[:], ALU.add)
         nc.scalar.activation(warm[:], rstd[:, N // P - 1 :], ACT.Gelu)
-        for c in range(NCHUNK):
-            aT_ps[c] = psum.tile([P, TB, F], F32, name=f"aT_ps{c}", tag="bank")
-            for j in range(TB):
-                tb = slice((c * TB + j) * P, (c * TB + j + 1) * P)
-                for cb in range(CB):
-                    nc.tensor.matmul(
-                        aT_ps[c][:, j, :], d[cb][:, tb], weights[:, cb, :], start=(cb == 0), stop=(cb == CB - 1)
-                    )
         h = held.tile([P, N], BF16, name="h", tag="var_h")
         a_ps = [psum.tile([P, CHUNK], F32, name=f"a_ps{c}", tag="bank") for c in range(NCHUNK)]
         for c in range(NCHUNK):

@@ -14,8 +14,8 @@ CHUNK = 512
 NCHUNK = N // CHUNK
 PIECE = 256
 NPIECE = N // PIECE
-TB = CHUNK // P
-LEAD = 2
+NTB = N // P
+GROUP = 3
 EPS = 1e-5
 
 FLOPS = 2 * N * C * F * 2
@@ -24,12 +24,13 @@ FLOPS = 2 * N * C * F * 2
 def tile_molecularretnet_kernel(tc, base, x, ln_w, ln_b, w1, b1, w2, b2, offs, out):
     nc = tc.nc
     chunks = [slice(t, t + CHUNK) for t in range(0, N, CHUNK)]
+    token_blocks = [slice(t, t + P) for t in range(0, N, P)]
+    groups = [list(range(j, min(j + GROUP, NTB))) for j in range(0, NTB, GROUP)]
     pieces = [slice(t, t + PIECE) for t in range(0, N, PIECE)]
     loads = pieces[:2] + chunks[1:]
     blocks = [slice(cb * P, (cb + 1) * P) for cb in range(CB)]
     with (
         tc.tile_pool(name="held", bufs=1) as held,
-        tc.tile_pool(name="small", bufs=2) as small,
         tc.psum_pool(name="psum", bufs=8) as psum,
     ):
         x_sb = [held.tile([P, N], F32, name=f"x_sb{cb}") for cb in range(CB)]
@@ -39,11 +40,9 @@ def tile_molecularretnet_kernel(tc, base, x, ln_w, ln_b, w1, b1, w2, b2, offs, o
         nc.scalar.dma_start(w1_sb[:], w1.rearrange("(b p) k -> p b k", p=P))
         ln_b_sb = held.tile([P, CB], F32, name="ln_b_sb")
         b1_sb = held.tile([P, 1], F32, name="b1_sb")
-        for step in range(len(loads) + LEAD):
-            if step < len(loads):
-                nc.sync.dma_start(x_sb[0][:, loads[step]], x[blocks[0], loads[step]])
-            if step >= LEAD:
-                nc.sync.dma_start(x_sb[1][:, loads[step - LEAD]], x[blocks[1], loads[step - LEAD]])
+        for cb in range(CB):
+            for tok in loads:
+                nc.sync.dma_start(x_sb[cb][:, tok], x[blocks[cb], tok])
         nc.sync.dma_start(ln_b_sb[:], ln_b.rearrange("(b p) o -> p (b o)", p=P))
         nc.sync.dma_start(b1_sb[:], b1)
         b2_sb = held.tile([P, CB], F32, name="b2_sb")
@@ -73,19 +72,24 @@ def tile_molecularretnet_kernel(tc, base, x, ln_w, ln_b, w1, b1, w2, b2, offs, o
             held.tile([P, N], BF16, name="squared0", tag="xb0_squared0"),
             held.tile([P, N], BF16, name="squared1"),
         ]
-        X0 = held.tile([P, N], F32, name="X0")
-        aT_scaled = held.tile([P, N // P, F], F32, name="aT_scaled", tag="aT_scaled_X1")
-        rstd = held.tile([P, N // P], F32, name="rstd")
-        var = held.tile([P, N // P], F32, name="var", tag="var_h")
+        aT_scaled = held.tile([P, NTB, F], F32, name="aT_scaled", tag="aT_scaled_X1")
+        rstd = held.tile([P, NTB], F32, name="rstd")
+        Ed2 = held.tile([P, NTB], F32, name="Ed2")
+        var = held.tile([P, NTB], F32, name="var", tag="var_h")
         f_b2 = [held.tile([P, N], F32, name=f"f_b2_{cb}") for cb in range(CB)]
         a_bias = held.tile([P, 1], F32, name="a_bias")
 
-        s_ps, aT_ps = {}, {}
+        X0 = held.tile([P, N], F32, name="X0")
+        for tok in loads:
+            nc.gpsimd.tensor_scalar_max(X0[:, tok], x_sb[0][:, tok], 0.0)
+
+        s_ps = {}
         for i, tok in enumerate(loads):
             nc.scalar.activation(xb0[:, tok], x_sb[0][:, tok], ACT.Relu)
             s_ps[i] = psum.tile([P, tok.stop - tok.start], F32, name=f"s_ps{i}", tag="bank")
             nc.tensor.matmul(s_ps[i][:], avg0[:], xb0[:, tok], start=True, stop=True)
-        weights = held.tile([P, CB, F], BF16, name="weights")
+        weights = held.tile([P, CB, F + 2], BF16, name="weights")
+        nc.vector.memset(weights[:, :, F:], 1.0 / C)
         w1_ln = held.tile([P, CB, F], BF16, name="w1_ln")
         for cb in range(CB):
             nc.vector.tensor_scalar_mul(w1_ln[:, cb, :], w1_sb[:, cb, :], ln_w_sb[:, cb : cb + 1])
@@ -94,7 +98,7 @@ def tile_molecularretnet_kernel(tc, base, x, ln_w, ln_b, w1, b1, w2, b2, offs, o
             nc.tensor.matmul(mean_w[:], avg[:], w1_ln[:, cb, :], start=(cb == 0), stop=(cb == CB - 1))
         for cb in range(CB):
             nc.vector.scalar_tensor_tensor(
-                weights[:, cb, :], w1_sb[:, cb, :], ln_w_sb[:, cb : cb + 1], mean_w[:], ALU.mult, ALU.subtract
+                weights[:, cb, :F], w1_sb[:, cb, :], ln_w_sb[:, cb : cb + 1], mean_w[:], ALU.mult, ALU.subtract
             )
         w1_f32 = held.tile([P, CB, F], F32, name="w1_f32")
         nc.gpsimd.tensor_copy(w1_f32[:], w1_sb[:])
@@ -103,60 +107,54 @@ def tile_molecularretnet_kernel(tc, base, x, ln_w, ln_b, w1, b1, w2, b2, offs, o
                 nc.vector.scalar_tensor_tensor(
                     d[cb][:, tok], x_sb[cb][:, tok], 0.0, s_ps[i][:], ALU.max, ALU.subtract
                 )
-            nc.scalar.activation(squared[0][:, tok], d[0][:, tok], ACT.Square)
-            nc.vector.tensor_tensor(squared[1][:, tok], d[1][:, tok], d[1][:, tok], ALU.mult)
-        for step in range(NCHUNK + 1):
-            if step < NCHUNK:
-                c = step
-                Ed = psum.tile([P, TB], F32, name=f"Ed{c}", tag="bank")
-                Ed2 = small.tile([P, TB], F32, name=f"Ed2_{c}", tag="Ed2")
-                d2 = psum.tile([P, TB], F32, name=f"d2_{c}", tag="bank")
-                for j in range(TB):
-                    tb = slice((c * TB + j) * P, (c * TB + j + 1) * P)
-                    for cb in range(CB):
-                        nc.tensor.matmul(
-                            Ed[:, j : j + 1], d[cb][:, tb], avg[:, 0:1], start=(cb == 0), stop=(cb == CB - 1)
-                        )
-                nc.scalar.activation(Ed2[:], Ed[:], ACT.Square)
-                for j in range(TB):
-                    tb = slice((c * TB + j) * P, (c * TB + j + 1) * P)
-                    for cb in range(CB):
-                        nc.tensor.matmul(
-                            d2[:, j : j + 1], squared[cb][:, tb], avg[:, 0:1], start=(cb == 0), stop=(cb == CB - 1)
-                        )
-                cols = slice(c * TB, (c + 1) * TB)
-                nc.vector.tensor_tensor(var[:, cols], d2[:], Ed2[:], ALU.subtract)
-                nc.scalar.activation(rstd[:, cols], var[:, cols], ACT.Abs_reciprocal_sqrt, bias=eps_col[:])
-            if step > 0:
-                c = step - 1
-                aT_ps[c] = psum.tile([P, TB, F], F32, name=f"aT_ps{c}", tag="bank")
-                for j in range(TB):
-                    tb = slice((c * TB + j) * P, (c * TB + j + 1) * P)
-                    for cb in range(CB):
-                        nc.tensor.matmul(
-                            aT_ps[c][:, j, :], d[cb][:, tb], weights[:, cb, :], start=(cb == 0), stop=(cb == CB - 1)
-                        )
+            for cb in range(CB):
+                if tok.stop < N:
+                    nc.scalar.activation(squared[cb][:, tok], d[cb][:, tok], ACT.Square)
+                else:
+                    nc.vector.tensor_tensor(squared[cb][:, tok], d[cb][:, tok], d[cb][:, tok], ALU.mult)
+        aT_ps = []
+        for g, blocks_g in enumerate(groups):
+            aT_ps.append(psum.tile([P, len(blocks_g), F + 2], F32, name=f"aT_ps{g}", tag="bank"))
+            for i, j in enumerate(blocks_g):
+                for cb in range(CB):
+                    nc.tensor.matmul(
+                        aT_ps[g][:, i, : F + 1], d[cb][:, token_blocks[j]], weights[:, cb, : F + 1],
+                        start=(cb == 0), stop=(cb == CB - 1),
+                    )
+            for i, j in enumerate(blocks_g):
+                for cb in range(CB):
+                    nc.tensor.matmul(
+                        aT_ps[g][:, i, F + 1 :], squared[cb][:, token_blocks[j]], avg[:, 0:1],
+                        start=(cb == 0), stop=(cb == CB - 1),
+                    )
+            cols = slice(blocks_g[0], blocks_g[-1] + 1)
+            nc.scalar.activation(Ed2[:, cols], aT_ps[g][:, :, F], ACT.Square)
+            nc.vector.tensor_tensor(var[:, cols], aT_ps[g][:, :, F + 1], Ed2[:, cols], ALU.subtract)
+            nc.scalar.activation(rstd[:, cols], var[:, cols], ACT.Abs_reciprocal_sqrt, bias=eps_col[:])
         bias_ps = psum.tile([P, 1], F32, name="bias_ps", tag="bank")
         for cb in range(CB):
             nc.tensor.matmul(
                 bias_ps[:], w1_f32[:, cb, :], ln_b_sb[:, cb : cb + 1], start=(cb == 0), stop=(cb == CB - 1)
             )
         nc.vector.tensor_tensor(a_bias[:], bias_ps[:], b1_sb[:], ALU.add)
-        nc.scalar.activation(warm[:], rstd[:, N // P - 1 :], ACT.Gelu)
+        nc.scalar.activation(warm[:], rstd[:, NTB - 1 :], ACT.Gelu)
         h = held.tile([P, N], BF16, name="h", tag="var_h")
-        a_ps = [psum.tile([P, CHUNK], F32, name=f"a_ps{c}", tag="bank") for c in range(NCHUNK)]
-        for c in range(NCHUNK):
-            for j in range(TB):
-                jj = c * TB + j
-                nc.vector.tensor_scalar_mul(aT_scaled[:, jj, :], aT_ps[c][:, j, :], rstd[:, jj : jj + 1])
-                nc.tensor.transpose(a_ps[c][:, j * P : (j + 1) * P], aT_scaled[:, jj, :], ident[:])
-        for k, tok in enumerate(pieces):
-            in_chunk = slice(k * PIECE % CHUNK, k * PIECE % CHUNK + PIECE)
-            nc.scalar.activation(h[:, tok], a_ps[k * PIECE // CHUNK][:, in_chunk], ACT.Gelu, bias=a_bias[:])
-            f_ps = psum.tile([P, PIECE], F32, name="f_ps0", tag="bank")
+        a_ps = []
+        for g, blocks_g in enumerate(groups):
+            n = len(blocks_g)
+            cols = slice(blocks_g[0], blocks_g[-1] + 1)
+            nc.vector.tensor_tensor(
+                aT_scaled[:, cols, :], aT_ps[g][:, :, :F], rstd[:, cols].unsqueeze(2).to_broadcast([P, n, F]), ALU.mult
+            )
+            a_ps.append(psum.tile([P, n * P], F32, name=f"a_ps{g}", tag="bank"))
+            for i, j in enumerate(blocks_g):
+                nc.tensor.transpose(a_ps[g][:, i * P : (i + 1) * P], aT_scaled[:, j, :], ident[:])
+        for g, blocks_g in enumerate(groups):
+            tok = slice(token_blocks[blocks_g[0]].start, token_blocks[blocks_g[-1]].stop)
+            nc.scalar.activation(h[:, tok], a_ps[g][:], ACT.Gelu, bias=a_bias[:])
+            f_ps = psum.tile([P, len(blocks_g) * P], F32, name="f_ps0", tag="bank")
             nc.tensor.matmul(f_ps[:], w2_sb[:, blocks[0]], h[:, tok], start=True, stop=True)
             nc.vector.tensor_scalar(f_b2[0][:, tok], f_ps[:], b2_sb[:, 0:1], None, ALU.add)
-            nc.scalar.activation(X0[:, tok], x_sb[0][:, tok], ACT.Relu)
         X1 = held.tile([P, N], F32, name="X1", tag="aT_scaled_X1")
         for tok in chunks:
             nc.scalar.activation(X1[:, tok], x_sb[1][:, tok], ACT.Relu)

@@ -79,6 +79,8 @@ def tile_molecularretnet_kernel(tc, base, x, ln_w, ln_b, w1, b1, w2, b2, offs, o
         f_b2 = [held.tile([P, N], F32, name=f"f_b2_{cb}") for cb in range(CB)]
         a_bias = held.tile([P, 1], F32, name="a_bias")
 
+        w1_f32 = held.tile([P, CB, F], F32, name="w1_f32")
+        nc.gpsimd.tensor_copy(w1_f32[:], w1_sb[:])
         X0 = held.tile([P, N], F32, name="X0")
         for tok in loads:
             nc.gpsimd.tensor_scalar_max(X0[:, tok], x_sb[0][:, tok], 0.0)
@@ -100,8 +102,6 @@ def tile_molecularretnet_kernel(tc, base, x, ln_w, ln_b, w1, b1, w2, b2, offs, o
             nc.vector.scalar_tensor_tensor(
                 weights[:, cb, :F], w1_sb[:, cb, :], ln_w_sb[:, cb : cb + 1], mean_w[:], ALU.mult, ALU.subtract
             )
-        w1_f32 = held.tile([P, CB, F], F32, name="w1_f32")
-        nc.gpsimd.tensor_copy(w1_f32[:], w1_sb[:])
         for i, tok in enumerate(loads):
             for cb in range(CB):
                 nc.vector.scalar_tensor_tensor(

@@ -70,7 +70,7 @@ def tile_molecularretnet_kernel(tc, base, x, ln_w, ln_b, w1, b1, w2, b2, offs, o
         xb0 = held.tile([P, N], BF16, name="xb0", tag="xb0_squared0")
         squared = [
             held.tile([P, N], BF16, name="squared0", tag="xb0_squared0"),
-            held.tile([P, N], BF16, name="squared1"),
+            held.tile([P, N], BF16, name="squared1", tag="squared1_X0"),
         ]
         aT_scaled = held.tile([P, NTB, F], F32, name="aT_scaled", tag="aT_scaled_X1")
         rstd = held.tile([P, NTB], F32, name="rstd")
@@ -81,9 +81,6 @@ def tile_molecularretnet_kernel(tc, base, x, ln_w, ln_b, w1, b1, w2, b2, offs, o
 
         w1_f32 = held.tile([P, CB, F], F32, name="w1_f32")
         nc.gpsimd.tensor_copy(w1_f32[:], w1_sb[:])
-        X0 = held.tile([P, N], F32, name="X0")
-        for tok in loads:
-            nc.gpsimd.tensor_scalar_max(X0[:, tok], x_sb[0][:, tok], 0.0)
 
         s_ps = {}
         for i, tok in enumerate(loads):
@@ -149,6 +146,9 @@ def tile_molecularretnet_kernel(tc, base, x, ln_w, ln_b, w1, b1, w2, b2, offs, o
             a_ps.append(psum.tile([P, n * P], F32, name=f"a_ps{g}", tag="bank"))
             for i, j in enumerate(blocks_g):
                 nc.tensor.transpose(a_ps[g][:, i * P : (i + 1) * P], aT_scaled[:, j, :], ident[:])
+        X0 = held.tile([P, N], F32, name="X0", tag="squared1_X0")
+        for tok in chunks:
+            nc.vector.tensor_scalar_max(X0[:, tok], x_sb[0][:, tok], 0.0)
         for g, blocks_g in enumerate(groups):
             tok = slice(token_blocks[blocks_g[0]].start, token_blocks[blocks_g[-1]].stop)
             nc.scalar.activation(h[:, tok], a_ps[g][:], ACT.Gelu, bias=a_bias[:])

@@ -87,18 +87,19 @@ def tile_molecularretnet_kernel(tc, base, x, ln_w, ln_b, w1, b1, w2, b2, offs, o
             nc.scalar.activation(xb0[:, tok], x_sb[0][:, tok], ACT.Relu)
             s_ps[i] = psum.tile([P, tok.stop - tok.start], F32, name=f"s_ps{i}", tag="bank")
             nc.tensor.matmul(s_ps[i][:], avg0[:], xb0[:, tok], start=True, stop=True)
-        weights = held.tile([P, CB, F + 2], BF16, name="weights")
-        nc.vector.memset(weights[:, :, F:], 1.0 / C)
-        w1_ln = held.tile([P, CB, F], BF16, name="w1_ln")
-        for cb in range(CB):
-            nc.vector.tensor_scalar_mul(w1_ln[:, cb, :], w1_sb[:, cb, :], ln_w_sb[:, cb : cb + 1])
-        mean_w = psum.tile([P, F], F32, name="mean_w", tag="bank")
-        for cb in range(CB):
-            nc.tensor.matmul(mean_w[:], avg[:], w1_ln[:, cb, :], start=(cb == 0), stop=(cb == CB - 1))
-        for cb in range(CB):
-            nc.vector.scalar_tensor_tensor(
-                weights[:, cb, :F], w1_sb[:, cb, :], ln_w_sb[:, cb : cb + 1], mean_w[:], ALU.mult, ALU.subtract
-            )
+            if tok.stop == CHUNK:
+                weights = held.tile([P, CB, F + 2], BF16, name="weights")
+                nc.vector.memset(weights[:, :, F:], 1.0 / C)
+                w1_ln = held.tile([P, CB, F], BF16, name="w1_ln")
+                for cb in range(CB):
+                    nc.vector.tensor_scalar_mul(w1_ln[:, cb, :], w1_sb[:, cb, :], ln_w_sb[:, cb : cb + 1])
+                mean_w = psum.tile([P, F], F32, name="mean_w", tag="bank")
+                for cb in range(CB):
+                    nc.tensor.matmul(mean_w[:], avg[:], w1_ln[:, cb, :], start=(cb == 0), stop=(cb == CB - 1))
+                for cb in range(CB):
+                    nc.vector.scalar_tensor_tensor(
+                        weights[:, cb, :F], w1_sb[:, cb, :], ln_w_sb[:, cb : cb + 1], mean_w[:], ALU.mult, ALU.subtract
+                    )
         for i, tok in enumerate(loads):
             for cb in range(CB):
                 nc.vector.scalar_tensor_tensor(

@@ -16,6 +16,7 @@ PIECE = 256
 NPIECE = N // PIECE
 NTB = N // P
 GROUP = 3
+LAG = 2
 EPS = 1e-5
 
 FLOPS = 2 * N * C * F * 2
@@ -138,24 +139,27 @@ def tile_molecularretnet_kernel(tc, base, x, ln_w, ln_b, w1, b1, w2, b2, offs, o
         nc.scalar.activation(warm[:], rstd[:, NTB - 1 :], ACT.Gelu)
         h = held.tile([P, N], BF16, name="h", tag="var_h")
         a_ps = []
-        for g, blocks_g in enumerate(groups):
-            n = len(blocks_g)
-            cols = slice(blocks_g[0], blocks_g[-1] + 1)
-            nc.vector.tensor_tensor(
-                aT_scaled[:, cols, :], aT_ps[g][:, :, :F], rstd[:, cols].unsqueeze(2).to_broadcast([P, n, F]), ALU.mult
-            )
-            a_ps.append(psum.tile([P, n * P], F32, name=f"a_ps{g}", tag="bank"))
-            for i, j in enumerate(blocks_g):
-                nc.tensor.transpose(a_ps[g][:, i * P : (i + 1) * P], aT_scaled[:, j, :], ident[:])
+        for step in range(len(groups) + LAG):
+            if step < len(groups):
+                g = step
+                cols = slice(groups[g][0], groups[g][-1] + 1)
+                n = len(groups[g])
+                nc.vector.tensor_tensor(
+                    aT_scaled[:, cols, :], aT_ps[g][:, :, :F], rstd[:, cols].unsqueeze(2).to_broadcast([P, n, F]), ALU.mult
+                )
+                a_ps.append(psum.tile([P, n * P], F32, name=f"a_ps{g}", tag="bank"))
+                for i, j in enumerate(groups[g]):
+                    nc.tensor.transpose(a_ps[g][:, i * P : (i + 1) * P], aT_scaled[:, j, :], ident[:])
+            if step >= LAG:
+                g = step - LAG
+                tok = slice(token_blocks[groups[g][0]].start, token_blocks[groups[g][-1]].stop)
+                nc.scalar.activation(h[:, tok], a_ps[g][:], ACT.Gelu, bias=a_bias[:])
+                f_ps = psum.tile([P, tok.stop - tok.start], F32, name="f_ps0", tag="bank")
+                nc.tensor.matmul(f_ps[:], w2_sb[:, blocks[0]], h[:, tok], start=True, stop=True)
+                nc.vector.tensor_scalar(f_b2[0][:, tok], f_ps[:], b2_sb[:, 0:1], None, ALU.add)
         X0 = held.tile([P, N], F32, name="X0", tag="squared1_X0")
         for tok in chunks:
             nc.vector.tensor_scalar_max(X0[:, tok], x_sb[0][:, tok], 0.0)
-        for g, blocks_g in enumerate(groups):
-            tok = slice(token_blocks[blocks_g[0]].start, token_blocks[blocks_g[-1]].stop)
-            nc.scalar.activation(h[:, tok], a_ps[g][:], ACT.Gelu, bias=a_bias[:])
-            f_ps = psum.tile([P, len(blocks_g) * P], F32, name="f_ps0", tag="bank")
-            nc.tensor.matmul(f_ps[:], w2_sb[:, blocks[0]], h[:, tok], start=True, stop=True)
-            nc.vector.tensor_scalar(f_b2[0][:, tok], f_ps[:], b2_sb[:, 0:1], None, ALU.add)
         X1 = held.tile([P, N], F32, name="X1", tag="aT_scaled_X1")
         for tok in chunks:
             nc.scalar.activation(X1[:, tok], x_sb[1][:, tok], ACT.Relu)

import concourse.mybir as mybir
from concourse.masks import make_identity

F32 = mybir.dt.float32
BF16 = mybir.dt.bfloat16
U16 = mybir.dt.uint16
ACT = mybir.ActivationFunctionType
ALU = mybir.AluOpType

P = 128
C, F, S, N = 256, 128, 4096, 2048
CB = C // P
CHUNK = 512
NCHUNK = N // CHUNK
PIECE = 256
NPIECE = N // PIECE
NTB = N // P
GROUP = 3
LAG = 2
EPS = 1e-5

FLOPS = 2 * N * C * F * 2


def tile_molecularretnet_kernel(tc, base, x, ln_w, ln_b, w1, b1, w2, b2, offs, out):
    nc = tc.nc
    chunks = [slice(t, t + CHUNK) for t in range(0, N, CHUNK)]
    token_blocks = [slice(t, t + P) for t in range(0, N, P)]
    groups = [list(range(j, min(j + GROUP, NTB))) for j in range(0, NTB, GROUP)]
    pieces = [slice(t, t + PIECE) for t in range(0, N, PIECE)]
    loads = pieces[:2] + chunks[1:]
    blocks = [slice(cb * P, (cb + 1) * P) for cb in range(CB)]
    with (
        tc.tile_pool(name="held", bufs=1) as held,
        tc.psum_pool(name="psum", bufs=8) as psum,
    ):
        x_sb = [held.tile([P, N], F32, name=f"x_sb{cb}") for cb in range(CB)]
        w1_sb = held.tile([P, CB, F], BF16, name="w1_sb")
        ln_w_sb = held.tile([P, CB], F32, name="ln_w_sb")
        nc.scalar.dma_start(ln_w_sb[:], ln_w.rearrange("(b p) o -> p (b o)", p=P))
        nc.scalar.dma_start(w1_sb[:], w1.rearrange("(b p) k -> p b k", p=P))
        ln_b_sb = held.tile([P, CB], F32, name="ln_b_sb")
        b1_sb = held.tile([P, 1], F32, name="b1_sb")
        for cb in range(CB):
            for tok in loads:
                nc.sync.dma_start(x_sb[cb][:, tok], x[blocks[cb], tok])
        nc.sync.dma_start(ln_b_sb[:], ln_b.rearrange("(b p) o -> p (b o)", p=P))
        nc.sync.dma_start(b1_sb[:], b1)
        b2_sb = held.tile([P, CB], F32, name="b2_sb")
        nc.sync.dma_start(b2_sb[:], b2.rearrange("(b p) o -> p (b o)", p=P))
        w2_sb = held.tile([P, C], BF16, name="w2_sb")
        nc.sync.dma_start(w2_sb[:], w2)
        offsets = held.tile([P, N // 16], U16, name="offsets")
        nc.sync.dma_start(offsets[:], offs)
        window = [held.tile([P, S], F32, name=f"window{cb}") for cb in range(CB)]
        for cb in range(CB):
            nc.sync.dma_start(window[cb][:], base[blocks[cb], :])

        avg0 = held.tile([P, P], BF16, name="avg0")
        nc.gpsimd.memset(avg0[:], 1.0 / P)
        avg = held.tile([P, P], BF16, name="avg")
        nc.gpsimd.memset(avg[:], 1.0 / C)
        eps_col = held.tile([P, 1], F32, name="eps_col")
        nc.gpsimd.memset(eps_col[:], EPS)
        ident = held.tile([P, P], F32, name="ident")
        make_identity(nc, ident[:])
        warm = held.tile([P, 1], F32, name="warm")
        nc.scalar.activation(warm[:], eps_col[:], ACT.Abs_reciprocal_sqrt)

        d = [held.tile([P, N], BF16, name=f"d{cb}") for cb in range(CB)]
        xb0 = held.tile([P, N], BF16, name="xb0", tag="xb0_squared0")
        squared = [
            held.tile([P, N], BF16, name="squared0", tag="xb0_squared0"),
            held.tile([P, N], BF16, name="squared1", tag="squared1_X0"),
        ]
        aT_scaled = held.tile([P, NTB, F], F32, name="aT_scaled", tag="aT_scaled_X1")
        rstd = held.tile([P, NTB], F32, name="rstd")
        Ed2 = held.tile([P, NTB], F32, name="Ed2")
        var = held.tile([P, NTB], F32, name="var", tag="var_h")
        f_b2 = [held.tile([P, N], F32, name=f"f_b2_{cb}") for cb in range(CB)]
        a_bias = held.tile([P, 1], F32, name="a_bias")

        w1_f32 = held.tile([P, CB, F], F32, name="w1_f32")
        nc.gpsimd.tensor_copy(w1_f32[:], w1_sb[:])

        s_ps = {}
        for i, tok in enumerate(loads):
            nc.scalar.activation(xb0[:, tok], x_sb[0][:, tok], ACT.Relu)
            s_ps[i] = psum.tile([P, tok.stop - tok.start], F32, name=f"s_ps{i}", tag="bank")
            nc.tensor.matmul(s_ps[i][:], avg0[:], xb0[:, tok], start=True, stop=True)
            if tok.stop == CHUNK:
                weights = held.tile([P, CB, F + 2], BF16, name="weights")
                nc.vector.memset(weights[:, :, F:], 1.0 / C)
                w1_ln = held.tile([P, CB, F], BF16, name="w1_ln")
                for cb in range(CB):
                    nc.vector.tensor_scalar_mul(w1_ln[:, cb, :], w1_sb[:, cb, :], ln_w_sb[:, cb : cb + 1])
                mean_w = psum.tile([P, F], F32, name="mean_w", tag="bank")
                for cb in range(CB):
                    nc.tensor.matmul(mean_w[:], avg[:], w1_ln[:, cb, :], start=(cb == 0), stop=(cb == CB - 1))
                for cb in range(CB):
                    nc.vector.scalar_tensor_tensor(
                        weights[:, cb, :F], w1_sb[:, cb, :], ln_w_sb[:, cb : cb + 1], mean_w[:], ALU.mult, ALU.subtract
                    )
        for i, tok in enumerate(loads):
            for cb in range(CB):
                nc.vector.scalar_tensor_tensor(
                    d[cb][:, tok], x_sb[cb][:, tok], 0.0, s_ps[i][:], ALU.max, ALU.subtract
                )
            for cb in range(CB):
                if tok.stop < N:
                    nc.scalar.activation(squared[cb][:, tok], d[cb][:, tok], ACT.Square)
                else:
                    nc.vector.tensor_tensor(squared[cb][:, tok], d[cb][:, tok], d[cb][:, tok], ALU.mult)
        aT_ps = []
        for g, blocks_g in enumerate(groups):
            aT_ps.append(psum.tile([P, len(blocks_g), F + 2], F32, name=f"aT_ps{g}", tag="bank"))
            for i, j in enumerate(blocks_g):
                for cb in range(CB):
                    nc.tensor.matmul(
                        aT_ps[g][:, i, : F + 1], d[cb][:, token_blocks[j]], weights[:, cb, : F + 1],
                        start=(cb == 0), stop=(cb == CB - 1),
                    )
            for i, j in enumerate(blocks_g):
                for cb in range(CB):
                    nc.tensor.matmul(
                        aT_ps[g][:, i, F + 1 :], squared[cb][:, token_blocks[j]], avg[:, 0:1],
                        start=(cb == 0), stop=(cb == CB - 1),
                    )
            cols = slice(blocks_g[0], blocks_g[-1] + 1)
            nc.scalar.activation(Ed2[:, cols], aT_ps[g][:, :, F], ACT.Square)
            nc.vector.tensor_tensor(var[:, cols], aT_ps[g][:, :, F + 1], Ed2[:, cols], ALU.subtract)
            nc.scalar.activation(rstd[:, cols], var[:, cols], ACT.Abs_reciprocal_sqrt, bias=eps_col[:])
        bias_ps = psum.tile([P, 1], F32, name="bias_ps", tag="bank")
        for cb in range(CB):
            nc.tensor.matmul(
                bias_ps[:], w1_f32[:, cb, :], ln_b_sb[:, cb : cb + 1], start=(cb == 0), stop=(cb == CB - 1)
            )
        nc.vector.tensor_tensor(a_bias[:], bias_ps[:], b1_sb[:], ALU.add)
        nc.scalar.activation(warm[:], rstd[:, NTB - 1 :], ACT.Gelu)
        h = held.tile([P, N], BF16, name="h", tag="var_h")
        a_ps = []
        for step in range(len(groups) + LAG):
            if step < len(groups):
                g = step
                cols = slice(groups[g][0], groups[g][-1] + 1)
                n = len(groups[g])
                nc.vector.tensor_tensor(
                    aT_scaled[:, cols, :], aT_ps[g][:, :, :F], rstd[:, cols].unsqueeze(2).to_broadcast([P, n, F]), ALU.mult
                )
                a_ps.append(psum.tile([P, n * P], F32, name=f"a_ps{g}", tag="bank"))
                for i, j in enumerate(groups[g]):
                    nc.tensor.transpose(a_ps[g][:, i * P : (i + 1) * P], aT_scaled[:, j, :], ident[:])
            if step >= LAG:
                g = step - LAG
                tok = slice(token_blocks[groups[g][0]].start, token_blocks[groups[g][-1]].stop)
                nc.scalar.activation(h[:, tok], a_ps[g][:], ACT.Gelu, bias=a_bias[:])
                f_ps = psum.tile([P, tok.stop - tok.start], F32, name="f_ps0", tag="bank")
                nc.tensor.matmul(f_ps[:], w2_sb[:, blocks[0]], h[:, tok], start=True, stop=True)
                nc.vector.tensor_scalar(f_b2[0][:, tok], f_ps[:], b2_sb[:, 0:1], None, ALU.add)
        X0 = held.tile([P, N], F32, name="X0", tag="squared1_X0")
        for tok in chunks:
            nc.vector.tensor_scalar_max(X0[:, tok], x_sb[0][:, tok], 0.0)
        X1 = held.tile([P, N], F32, name="X1", tag="aT_scaled_X1")
        for tok in chunks:
            nc.scalar.activation(X1[:, tok], x_sb[1][:, tok], ACT.Relu)
            f_ps = psum.tile([P, CHUNK], F32, name="f_ps1", tag="bank")
            nc.tensor.matmul(f_ps[:], w2_sb[:, blocks[1]], h[:, tok], start=True, stop=True)
            nc.scalar.activation(f_b2[1][:, tok], f_ps[:], ACT.Identity, bias=b2_sb[:, 1:2])

        X = [X0, X1]
        for cb in range(CB):
            nc.vector.tensor_tensor(window[cb][:].indirect(offsets[:]), f_b2[cb][:], X[cb][:], ALU.add)
            nc.sync.dma_start(out[blocks[cb], 0 : S // 2], window[cb][:, 0 : S // 2])
            nc.scalar.dma_start(out[blocks[cb], S // 2 : S], window[cb][:, S // 2 : S])
